import numpy as np
import ml_dtypes


def mxq(x, axis, fmt="e4m3"):
    dtype, down = {"e4m3": (ml_dtypes.float8_e4m3fn, 7), "e5m2": (ml_dtypes.float8_e5m2, 14)}[fmt]
    v = np.moveaxis(np.asarray(x, np.float32).astype(ml_dtypes.bfloat16).astype(np.float64), axis, -1)
    blocks = v.reshape(v.shape[:-1] + (-1, 32))
    amax = np.abs(blocks).max(-1, keepdims=True)
    byte = np.maximum(np.where(amax > 0, np.frexp(amax)[1] - 1 + 127, 0) - down, 1)
    scale = np.exp2(byte - 127.0)
    codes = (blocks / scale).astype(np.float32).astype(dtype).astype(np.float64)
    return np.moveaxis((codes * scale).reshape(v.shape), -1, axis)


WIDE = False


def mx_kscale(k):
    if not WIDE:
        return np.ones(k)
    levels = np.array([10, -10, 5, -5, 0])
    a = np.random.permutation(np.resize(levels, k // 512 * 4)).reshape(k // 512, 4)
    idx = np.arange(k)
    return np.exp2(a[idx // 512, idx % 128 // 32])


BF16 = ml_dtypes.bfloat16


def bf(x):
    return np.asarray(x, np.float32).astype(BF16)


def f64(x):
    return np.asarray(x).astype(np.float64)


E2M1 = np.array([0.0, 0.5, 1.0, 1.5, 2.0, 3.0, 4.0, 6.0, -0.0, -0.5, -1.0, -1.5, -2.0, -3.0, -4.0, -6.0])


def pack_weight(w, fmt):
    k, n = w.shape
    w = f64(bf(w)).reshape(k // 32, 32, n)
    amax = np.abs(w).max(1)
    if fmt == "e4m3":
        byte = np.frexp(amax)[1] - 1 + 127 - 7
    else:
        mant, ex = np.frexp(amax / 6.0)
        byte = np.where(mant > 0.5, ex, ex - 1) + 127
    byte = np.clip(np.where(amax > 0, byte, 1), 1, 254)
    scaled = (w * np.exp2(127.0 - byte)[:, None, :]).reshape(k, n).astype(np.float32)
    by_word = np.ascontiguousarray(scaled.reshape(k // 512, 128, 4, n).transpose(0, 1, 3, 2))
    if fmt == "e4m3":
        words = by_word.astype(ml_dtypes.float8_e4m3fn).view(np.uint8)
    else:
        c = by_word.astype(ml_dtypes.float4_e2m1fn).view(np.uint8) & 0xF
        words = c[..., 0::2] | (c[..., 1::2] << 4)
    return np.ascontiguousarray(words), np.ascontiguousarray(byte.astype(np.uint8).reshape(k // 512, 16, n))


def unpack_weight(words, scales, fmt):
    g, p, n, _ = words.shape
    if fmt == "e4m3":
        vals = np.ascontiguousarray(words).view(ml_dtypes.float8_e4m3fn).astype(np.float64)
    else:
        nib = np.empty((g, p, n, 4), np.uint8)
        nib[..., 0::2] = words & 0xF
        nib[..., 1::2] = words >> 4
        vals = E2M1[nib]
    vals = vals * np.repeat(np.exp2(scales.astype(np.float64) - 127.0), 8, axis=1)[..., None]
    return vals.transpose(0, 1, 3, 2).reshape(g * 512, n)


B, CIN, R, COUT, H, W, D, KS = 1, 2048, 2048, 2048, 8, 4, 4, 3
P = H * W * D
PAD = (KS - 1) // 2
FMT = "e4m3"


def slice_in_dim(t, a, b, axis):
    idx = [slice(None)] * t.ndim
    idx[axis] = slice(a, b)
    return t[tuple(idx)]


def axis_contract(t, U, axis):
    L = t.shape[axis] - (KS - 1)
    rshape = (1, U.shape[1], 1, 1, 1)
    acc = slice_in_dim(t, 0, L, axis) * U[0].reshape(rshape)
    for k in range(1, KS):
        acc = acc + slice_in_dim(t, k, k + L, axis) * U[k].reshape(rshape)
    return acc


def setup_inputs():
    s, t = mx_kscale(CIN), mx_kscale(R)
    x = bf(np.random.standard_normal((B, CIN, H, W, D)) * s[None, :, None, None, None])
    U_kh = bf(np.random.standard_normal((KS, R)) / np.sqrt(KS))
    U_kw = bf(np.random.standard_normal((KS, R)) / np.sqrt(KS))
    U_kd = bf(np.random.standard_normal((KS, R)) / np.sqrt(KS))
    in_words, in_scales = pack_weight(np.random.standard_normal((CIN, R)) / np.sqrt(CIN) / s[:, None] * t[None, :], FMT)
    out_words, out_scales = pack_weight(np.random.standard_normal((R, COUT)) / np.sqrt(R) / t[:, None], FMT)
    bias = bf(np.random.standard_normal(COUT) * 0.5)
    return {"x": x,
            "U_kh": U_kh,
            "U_kw": U_kw,
            "U_kd": U_kd,
            "U_c_in_words": in_words,
            "U_c_in_scales": in_scales,
            "U_c_out_words": out_words,
            "U_c_out_scales": out_scales,
            "bias": bias}


def reference(x, U_kh, U_kw, U_kd, U_c_in_words, U_c_in_scales, U_c_out_words, U_c_out_scales, bias):
    xq = mxq(f64(x), 1, "e4m3").reshape(B, CIN, P)
    y = (unpack_weight(U_c_in_words, U_c_in_scales, FMT).T @ xq).reshape(B, R, H, W, D)
    y = np.pad(y, ((0, 0), (0, 0), (PAD, PAD), (PAD, PAD), (PAD, PAD)))
    y = axis_contract(y, f64(U_kh), 2)
    y = axis_contract(y, f64(U_kw), 3)
    y = axis_contract(y, f64(U_kd), 4)
    out = (unpack_weight(U_c_out_words, U_c_out_scales, FMT).T @ mxq(y, 1, "e4m3").reshape(B, R, P)).reshape(B, COUT, H, W, D)
    return out + f64(bias)[None, :, None, None, None]

@@ -1,0 +1,252 @@
+from contextlib import ExitStack
+
+import concourse.mybir as mybir
+from concourse.masks import make_identity
+
+F32 = mybir.dt.float32
+BF16 = mybir.dt.bfloat16
+I32 = mybir.dt.int32
+U32 = mybir.dt.uint32
+U8 = mybir.dt.uint8
+FP8X4 = mybir.dt.float8_e4m3fn_x4
+MULT = mybir.AluOpType.mult
+ADD = mybir.AluOpType.add
+COPY = mybir.ActivationFunctionType.Copy
+IDENTITY = mybir.ActivationFunctionType.Identity
+
+P = 128
+PACK = 4
+K_PASS = P * PACK
+CHANNELS = 2048
+GROUPS = CHANNELS // K_PASS
+H, W, D = 8, 4, 4
+POS = H * W * D
+TAPS = 3
+AXIS_H, AXIS_W, AXIS_D = 0, 1, 2
+BIAS_ROW = 3 * TAPS * GROUPS
+VECTOR_ROWS = BIAS_ROW + GROUPS
+
+FLOPS = 2 * 2 * POS * CHANNELS * CHANNELS + 2 * 3 * TAPS * POS * CHANNELS
+
+
+def load_scale_planes(nc, planes, scales):
+    for quad in range(4):
+        nc.sync.dma_start(
+            out=planes[32 * quad : 32 * quad + 16, :].bitcast(I32),
+            in_=scales[:, 4 * quad : 4 * quad + 4, :].bitcast(I32),
+        )
+
+
+def tile_lowrankconv3d_w_kernel(
+    tc, x, U_kh, U_kw, U_kd, U_c_in_words, U_c_in_scales, U_c_out_words, U_c_out_scales, bias, out
+):
+    nc = tc.nc
+    with ExitStack() as ctx:
+        keep = ctx.enter_context(tc.tile_pool(name="keep", bufs=1))
+        work = ctx.enter_context(tc.tile_pool(name="work", bufs=2))
+        results = ctx.enter_context(tc.tile_pool(name="results", bufs=GROUPS))
+        banks = ctx.enter_context(tc.psum_pool(name="banks", bufs=4))
+        sums = ctx.enter_context(tc.psum_pool(name="sums", bufs=1))
+
+        x_raw = keep.tile([P, GROUPS, PACK, POS], BF16)
+        nc.sync.dma_start(
+            out=x_raw[:], in_=x.rearrange("b (g p t) h w d -> p (b g) t (h w d)", p=P, t=PACK)
+        )
+
+        in_planes = keep.tile([P, CHANNELS], U8, align_bytes=64)
+        out_planes = keep.tile([P, CHANNELS], U8, align_bytes=64)
+        nc.vector.memset(in_planes[:].bitcast(I32), 0)
+        nc.vector.memset(out_planes[:].bitcast(I32), 0)
+        vectors = keep.tile([P, K_PASS], BF16)
+        nc.vector.memset(vectors[:], 0.0)
+
+        load_scale_planes(nc, in_planes, U_c_in_scales)
+        w_in = []
+        for g in range(GROUPS):
+            w_in.append(keep.tile([P, GROUPS, K_PASS], I32, name="w_in%d" % g, align_bytes=64))
+            for k in range(GROUPS):
+                words = U_c_in_words[k].rearrange("p n t -> p (n t)")
+                nc.sync.dma_start(
+                    out=w_in[g][:, k, :],
+                    in_=words[:, PACK * K_PASS * g : PACK * K_PASS * (g + 1)].bitcast(I32),
+                )
+        load_scale_planes(nc, out_planes, U_c_out_scales)
+        w_out = []
+        for g in range(GROUPS):
+            w_out.append(keep.tile([P, CHANNELS], I32, name="w_out%d" % g, align_bytes=64))
+            nc.sync.dma_start(
+                out=w_out[g][:], in_=U_c_out_words[g].rearrange("p n t -> p (n t)").bitcast(I32)
+            )
+
+        for axis, taps in enumerate((U_kh, U_kw, U_kd)):
+            first = axis * TAPS * GROUPS
+            nc.scalar.dma_start(
+                out=vectors[first : first + TAPS * GROUPS, :],
+                in_=taps.rearrange("k (g c) -> (k g) c", g=GROUPS),
+            )
+        nc.scalar.dma_start(
+            out=vectors[BIAS_ROW:VECTOR_ROWS, :], in_=bias.rearrange("(g c) -> g c", g=GROUPS)
+        )
+
+        ident_bf = keep.tile([P, P], BF16)
+        make_identity(nc, ident_bf[:])
+        ident = keep.tile([P, P], F32)
+        make_identity(nc, ident[:])
+        from_below = keep.tile([P, POS], F32)
+        from_above = keep.tile([P, POS], F32)
+        nc.vector.memset(from_below[:], 0.0)
+        nc.vector.memset(from_above[:], 0.0)
+        ident_d = ident[:].rearrange("i (e d) -> i e d", d=D)
+        nc.vector.tensor_copy(
+            out=from_below[:].rearrange("i (e d) -> i e d", d=D)[:, :, 1:D], in_=ident_d[:, :, 0 : D - 1]
+        )
+        nc.vector.tensor_copy(
+            out=from_above[:].rearrange("i (e d) -> i e d", d=D)[:, :, 0 : D - 1], in_=ident_d[:, :, 1:D]
+        )
+
+        vectors_turned = banks.tile([P, PACK, P], BF16, tag="bank")
+        for t in range(PACK):
+            nc.tensor.transpose(vectors_turned[:, t, :], vectors[:, t:K_PASS:PACK], ident_bf[:])
+        per_rank = keep.tile([P, PACK, VECTOR_ROWS], F32)
+        nc.scalar.activation(out=per_rank[:], in_=vectors_turned[:, :, 0:VECTOR_ROWS], func=COPY)
+
+        def tap(axis, k, g, t):
+            row = (axis * TAPS + k) * GROUPS + g
+            return per_rank[:, t, row : row + 1]
+
+        x_grouped = keep.tile([P, GROUPS, POS, PACK], BF16, align_bytes=64)
+        x_words = keep.tile([P, GROUPS, POS], U32, align_bytes=64)
+        x_scales = keep.tile([P, GROUPS, POS], U8, align_bytes=64)
+        for k in range(GROUPS):
+            nc.vector.tensor_copy(out=x_grouped[:, k], in_=x_raw[:, k].rearrange("p t n -> p n t"))
+        for k in range(GROUPS):
+            nc.vector.quantize_mx(
+                out=x_words[:, k, :].bitcast(FP8X4),
+                scales=x_scales[:, k, :],
+                in_=x_grouped[:, k].rearrange("p n t -> p (n t)"),
+            )
+
+        y3_words = keep.tile([P, GROUPS, POS], U32, align_bytes=64)
+        y3_scales = keep.tile([P, GROUPS, POS], U8, align_bytes=64)
+
+        def sort_by_byte(copy, bank):
+            by_byte = work.tile([P, PACK, P], F32, tag="by_byte")
+            copy(out=by_byte[:], in_=bank[:].rearrange("n (p t) -> n t p", t=PACK))
+            return by_byte
+
+        def ranks_of_group(g):
+            y0 = banks.tile([P, K_PASS], F32, tag="bank")
+            for k in range(GROUPS):
+                nc.tensor.matmul_mx(
+                    out=y0[:],
+                    lhsT=x_words[:, k, :].bitcast(FP8X4),
+                    lhsT_scale=x_scales[:, k, :],
+                    rhs=w_in[g][:, k, :].bitcast(FP8X4),
+                    rhs_scale=in_planes[PACK * k : P, K_PASS * g : K_PASS * (g + 1)],
+                    start=(k == 0),
+                    stop=(k == GROUPS - 1),
+                )
+            by_byte = sort_by_byte(nc.scalar.copy, y0)
+            turned = []
+            for matrix in (ident, from_below, from_above):
+                bank = banks.tile([P, PACK, POS], F32, tag="bank")
+                for t in range(PACK):
+                    nc.tensor.transpose(bank[:, t, :], by_byte[:, t, :], matrix[:])
+                turned.append(bank)
+            return turned
+
+        def middle_tap(dst, src, axis, g):
+            for t in range(PACK):
+                nc.scalar.activation(
+                    out=dst[:, t, :], in_=src[:, t, :], func=COPY, scale=tap(axis, 1, g, t)
+                )
+
+        def add_tap(dst, src, scalar):
+            nc.vector.scalar_tensor_tensor(
+                out=dst, in0=src, scalar=scalar, in1=dst, op0=MULT, op1=ADD
+            )
+
+        def filter_in_sbuf(src, axis, g, step, length):
+            dst = work.tile([P, PACK, POS], F32, tag="filtered%d" % axis)
+            middle_tap(dst, src, axis, g)
+            run = step * length
+            for k in (0, 2):
+                for t in range(PACK):
+                    to = dst[:, t, :].rearrange("p (a e) -> p a e", e=run)
+                    frm = src[:, t, :].rearrange("p (a e) -> p a e", e=run)
+                    if k == 0:
+                        add_tap(to[:, :, step:run], frm[:, :, 0 : run - step], tap(axis, k, g, t))
+                    else:
+                        add_tap(to[:, :, 0 : run - step], frm[:, :, step:run], tap(axis, k, g, t))
+            return dst
+
+        def group_bytes(y3):
+            grouped = work.tile([P, POS, PACK], BF16, tag="grouped", align_bytes=64)
+            nc.scalar.copy(out=grouped[:], in_=y3[:].rearrange("p t n -> p n t"))
+            return grouped
+
+        def quantise(g, grouped):
+            nc.vector.quantize_mx(
+                out=y3_words[:, g, :].bitcast(FP8X4),
+                scales=y3_scales[:, g, :],
+                in_=grouped[:].rearrange("p n t -> p (n t)"),
+            )
+
+        turned = ranks_of_group(0)
+        y3 = None
+        grouped = None
+        for g in range(GROUPS):
+            middle, below, above = turned
+            y1 = work.tile([P, PACK, POS], F32, tag="filtered%d" % AXIS_D)
+            middle_tap(y1, middle, AXIS_D, g)
+            if g > 0:
+                grouped = group_bytes(y3)
+            for t in range(PACK):
+                add_tap(y1[:, t, :], below[:, t, :], tap(AXIS_D, 0, g, t))
+            for t in range(PACK):
+                add_tap(y1[:, t, :], above[:, t, :], tap(AXIS_D, 2, g, t))
+            if g > 0:
+                quantise(g - 1, grouped)
+            if g + 1 < GROUPS:
+                turned = ranks_of_group(g + 1)
+            y2 = filter_in_sbuf(y1, AXIS_W, g, D, W)
+            y3 = filter_in_sbuf(y2, AXIS_H, g, W * D, H)
+        quantise(GROUPS - 1, group_bytes(y3))
+
+        out_sums = [sums.tile([P, K_PASS], F32, name="out_sum%d" % b) for b in range(GROUPS)]
+        for g in range(GROUPS):
+            for b in range(GROUPS):
+                nc.tensor.matmul_mx(
+                    out=out_sums[b][:],
+                    lhsT=y3_words[:, g, :].bitcast(FP8X4),
+                    lhsT_scale=y3_scales[:, g, :],
+                    rhs=w_out[g][:, K_PASS * b : K_PASS * (b + 1)].bitcast(FP8X4),
+                    rhs_scale=out_planes[PACK * g : P, K_PASS * b : K_PASS * (b + 1)],
+                    start=(g == 0),
+                    stop=(g == GROUPS - 1),
+                )
+
+        out_blocks = out.rearrange("a (b p t) h w d -> b p (a t h w d)", p=P, t=PACK)
+        for b in range(GROUPS):
+            on_scalar = b % 2 == 0
+            by_byte = sort_by_byte(nc.scalar.copy if on_scalar else nc.vector.tensor_copy, out_sums[b])
+            bank = banks.tile([P, PACK, POS], F32, tag="bank")
+            for t in range(PACK):
+                nc.tensor.transpose(bank[:, t, :], by_byte[:, t, :], ident[:])
+            result = results.tile([P, PACK, POS], F32)
+            if on_scalar:
+                for t in range(PACK):
+                    nc.scalar.activation(
+                        out=result[:, t, :],
+                        in_=bank[:, t, :],
+                        func=IDENTITY,
+                        bias=per_rank[:, t, BIAS_ROW + b : BIAS_ROW + b + 1],
+                    )
+            else:
+                nc.vector.tensor_tensor(
+                    out=result[:],
+                    in0=bank[:],
+                    in1=per_rank[:, :, BIAS_ROW + b : BIAS_ROW + b + 1].to_broadcast([P, PACK, POS]),
+                    op=ADD,
+                )
+            nc.sync.dma_start(out=out_blocks[b], in_=result[:].rearrange("p t n -> p (t n)"))

@@ -19,6 +19,7 @@ PACK = 4
 K_PASS = P * PACK
 CHANNELS = 2048
 GROUPS = CHANNELS // K_PASS
+BLOCKS = CHANNELS // P
 H, W, D = 8, 4, 4
 POS = H * W * D
 TAPS = 3
@@ -45,20 +46,20 @@ def tile_lowrankconv3d_w_kernel(
         keep = ctx.enter_context(tc.tile_pool(name="keep", bufs=1))
         work = ctx.enter_context(tc.tile_pool(name="work", bufs=2))
         results = ctx.enter_context(tc.tile_pool(name="results", bufs=GROUPS))
-        banks = ctx.enter_context(tc.psum_pool(name="banks", bufs=4))
-        sums = ctx.enter_context(tc.psum_pool(name="sums", bufs=1))
+        banks = ctx.enter_context(tc.psum_pool(name="banks", bufs=8))
+        ctx.enter_context(tc.manual_schedule())
 
         x_raw = keep.tile([P, GROUPS, PACK, POS], BF16)
         nc.sync.dma_start(
             out=x_raw[:], in_=x.rearrange("b (g p t) h w d -> p (b g) t (h w d)", p=P, t=PACK)
         )
 
+        vectors = keep.tile([P, K_PASS], BF16)
+        nc.vector.memset(vectors[:], 0.0)
         in_planes = keep.tile([P, CHANNELS], U8, align_bytes=64)
         out_planes = keep.tile([P, CHANNELS], U8, align_bytes=64)
         nc.vector.memset(in_planes[:].bitcast(I32), 0)
         nc.vector.memset(out_planes[:].bitcast(I32), 0)
-        vectors = keep.tile([P, K_PASS], BF16)
-        nc.vector.memset(vectors[:], 0.0)
 
         load_scale_planes(nc, in_planes, U_c_in_scales)
         w_in = []
@@ -147,73 +148,81 @@ def tile_lowrankconv3d_w_kernel(
                     stop=(k == GROUPS - 1),
                 )
             by_byte = sort_by_byte(nc.scalar.copy, y0)
-            turned = []
+            three_banks = []
             for matrix in (ident, from_below, from_above):
                 bank = banks.tile([P, PACK, POS], F32, tag="bank")
                 for t in range(PACK):
                     nc.tensor.transpose(bank[:, t, :], by_byte[:, t, :], matrix[:])
-                turned.append(bank)
-            return turned
+                three_banks.append(bank)
+            return three_banks
 
-        def middle_tap(dst, src, axis, g):
-            for t in range(PACK):
-                nc.scalar.activation(
-                    out=dst[:, t, :], in_=src[:, t, :], func=COPY, scale=tap(axis, 1, g, t)
-                )
+        y1 = keep.tile([P, BLOCKS, POS], F32)
+        y2 = keep.tile([P, BLOCKS, POS], F32)
+        y3 = keep.tile([P, BLOCKS, POS], F32)
+        y3_grouped = keep.tile([P, GROUPS, POS, PACK], BF16, align_bytes=64)
+        turned = [ranks_of_group(0)]
 
-        def add_tap(dst, src, scalar):
+        def middle_tap(dst, src, axis, i):
+            g, t = divmod(i, PACK)
+            nc.scalar.activation(out=dst, in_=src, func=COPY, scale=tap(axis, 1, g, t))
+
+        def outer_tap(dst, src, axis, k, i):
+            g, t = divmod(i, PACK)
             nc.vector.scalar_tensor_tensor(
-                out=dst, in0=src, scalar=scalar, in1=dst, op0=MULT, op1=ADD
+                out=dst, in0=src, scalar=tap(axis, k, g, t), in1=dst, op0=MULT, op1=ADD
             )
 
-        def filter_in_sbuf(src, axis, g, step, length):
-            dst = work.tile([P, PACK, POS], F32, tag="filtered%d" % axis)
-            middle_tap(dst, src, axis, g)
+        def outer_tap_in_sbuf(dst, src, axis, k, i, step, length):
             run = step * length
+            to = dst[:, i, :].rearrange("p (a e) -> p a e", e=run)
+            frm = src[:, i, :].rearrange("p (a e) -> p a e", e=run)
+            if k == 0:
+                outer_tap(to[:, :, step:run], frm[:, :, 0 : run - step], axis, k, i)
+            else:
+                outer_tap(to[:, :, 0 : run - step], frm[:, :, step:run], axis, k, i)
+
+        GROUP_LAG = PACK - 1 + 5 + 1
+        QUANTISE_LAG = GROUP_LAG + 1
+
+        def is_block(i):
+            return 0 <= i < BLOCKS
+
+        def is_group_start(i):
+            return is_block(i) and i % PACK == 0
+
+        for j in range(BLOCKS - PACK + QUANTISE_LAG + 1):
+            if is_block(j):
+                g, t = divmod(j, PACK)
+                middle_tap(y1[:, j, :], turned[g][0][:, t, :], AXIS_D, j)
+            if is_block(j - 2):
+                middle_tap(y2[:, j - 2, :], y1[:, j - 2, :], AXIS_W, j - 2)
+            if is_block(j - 4):
+                middle_tap(y3[:, j - 4, :], y2[:, j - 4, :], AXIS_H, j - 4)
+            if is_group_start(j - GROUP_LAG):
+                g = (j - GROUP_LAG) // PACK
+                nc.scalar.copy(
+                    out=y3_grouped[:, g],
+                    in_=y3[:, PACK * g : PACK * (g + 1), :].rearrange("p t n -> p n t"),
+                )
             for k in (0, 2):
-                for t in range(PACK):
-                    to = dst[:, t, :].rearrange("p (a e) -> p a e", e=run)
-                    frm = src[:, t, :].rearrange("p (a e) -> p a e", e=run)
-                    if k == 0:
-                        add_tap(to[:, :, step:run], frm[:, :, 0 : run - step], tap(axis, k, g, t))
-                    else:
-                        add_tap(to[:, :, 0 : run - step], frm[:, :, step:run], tap(axis, k, g, t))
-            return dst
+                if is_block(j - 1):
+                    g, t = divmod(j - 1, PACK)
+                    outer_tap(y1[:, j - 1, :], turned[g][1 + k // 2][:, t, :], AXIS_D, k, j - 1)
+                if is_block(j - 3):
+                    outer_tap_in_sbuf(y2, y1, AXIS_W, k, j - 3, D, W)
+                if is_block(j - 5):
+                    outer_tap_in_sbuf(y3, y2, AXIS_H, k, j - 5, W * D, H)
+            if is_group_start(j - QUANTISE_LAG):
+                g = (j - QUANTISE_LAG) // PACK
+                nc.vector.quantize_mx(
+                    out=y3_words[:, g, :].bitcast(FP8X4),
+                    scales=y3_scales[:, g, :],
+                    in_=y3_grouped[:, g].rearrange("p n t -> p (n t)"),
+                )
+            if is_group_start(j) and j // PACK + 1 < GROUPS:
+                turned.append(ranks_of_group(j // PACK + 1))
 
-        def group_bytes(y3):
-            grouped = work.tile([P, POS, PACK], BF16, tag="grouped", align_bytes=64)
-            nc.scalar.copy(out=grouped[:], in_=y3[:].rearrange("p t n -> p n t"))
-            return grouped
-
-        def quantise(g, grouped):
-            nc.vector.quantize_mx(
-                out=y3_words[:, g, :].bitcast(FP8X4),
-                scales=y3_scales[:, g, :],
-                in_=grouped[:].rearrange("p n t -> p (n t)"),
-            )
-
-        turned = ranks_of_group(0)
-        y3 = None
-        grouped = None
-        for g in range(GROUPS):
-            middle, below, above = turned
-            y1 = work.tile([P, PACK, POS], F32, tag="filtered%d" % AXIS_D)
-            middle_tap(y1, middle, AXIS_D, g)
-            if g > 0:
-                grouped = group_bytes(y3)
-            for t in range(PACK):
-                add_tap(y1[:, t, :], below[:, t, :], tap(AXIS_D, 0, g, t))
-            for t in range(PACK):
-                add_tap(y1[:, t, :], above[:, t, :], tap(AXIS_D, 2, g, t))
-            if g > 0:
-                quantise(g - 1, grouped)
-            if g + 1 < GROUPS:
-                turned = ranks_of_group(g + 1)
-            y2 = filter_in_sbuf(y1, AXIS_W, g, D, W)
-            y3 = filter_in_sbuf(y2, AXIS_H, g, W * D, H)
-        quantise(GROUPS - 1, group_bytes(y3))
-
-        out_sums = [sums.tile([P, K_PASS], F32, name="out_sum%d" % b) for b in range(GROUPS)]
+        out_sums = [banks.tile([P, K_PASS], F32, name="out_sum%d" % b, tag="bank") for b in range(GROUPS)]
         for g in range(GROUPS):
             for b in range(GROUPS):
                 nc.tensor.matmul_mx(

@@ -20,6 +20,8 @@ K_PASS = P * PACK
 CHANNELS = 2048
 GROUPS = CHANNELS // K_PASS
 BLOCKS = CHANNELS // P
+PER_ROUND = 2
+ROUNDS_PER_GROUP = PACK // PER_ROUND
 H, W, D = 8, 4, 4
 POS = H * W * D
 TAPS = 3
@@ -118,14 +120,17 @@ def tile_lowrankconv3d_w_kernel(
         x_grouped = keep.tile([P, GROUPS, POS, PACK], BF16, align_bytes=64)
         x_words = keep.tile([P, GROUPS, POS], U32, align_bytes=64)
         x_scales = keep.tile([P, GROUPS, POS], U8, align_bytes=64)
-        for k in range(GROUPS):
-            nc.vector.tensor_copy(out=x_grouped[:, k], in_=x_raw[:, k].rearrange("p t n -> p n t"))
-        for k in range(GROUPS):
-            nc.vector.quantize_mx(
-                out=x_words[:, k, :].bitcast(FP8X4),
-                scales=x_scales[:, k, :],
-                in_=x_grouped[:, k].rearrange("p n t -> p (n t)"),
-            )
+        for k in range(GROUPS + 1):
+            if k < GROUPS:
+                nc.vector.tensor_copy(
+                    out=x_grouped[:, k], in_=x_raw[:, k].rearrange("p t n -> p n t")
+                )
+            if k > 0:
+                nc.vector.quantize_mx(
+                    out=x_words[:, k - 1, :].bitcast(FP8X4),
+                    scales=x_scales[:, k - 1, :],
+                    in_=x_grouped[:, k - 1].rearrange("p n t -> p (n t)"),
+                )
 
         y3_words = keep.tile([P, GROUPS, POS], U32, align_bytes=64)
         y3_scales = keep.tile([P, GROUPS, POS], U8, align_bytes=64)
@@ -181,46 +186,45 @@ def tile_lowrankconv3d_w_kernel(
             else:
                 outer_tap(to[:, :, 0 : run - step], frm[:, :, step:run], axis, k, i)
 
-        GROUP_LAG = PACK - 1 + 5 + 1
-        QUANTISE_LAG = GROUP_LAG + 1
+        def blocks_of(entry_round):
+            first = entry_round * PER_ROUND
+            return [i for i in range(first, first + PER_ROUND) if 0 <= i < BLOCKS]
 
-        def is_block(i):
-            return 0 <= i < BLOCKS
+        def group_ending(entry_round):
+            g, rest = divmod(entry_round + 1, ROUNDS_PER_GROUP)
+            return g - 1 if rest == 0 and 1 <= g <= GROUPS else None
 
-        def is_group_start(i):
-            return is_block(i) and i % PACK == 0
-
-        for j in range(BLOCKS - PACK + QUANTISE_LAG + 1):
-            if is_block(j):
-                g, t = divmod(j, PACK)
-                middle_tap(y1[:, j, :], turned[g][0][:, t, :], AXIS_D, j)
-            if is_block(j - 2):
-                middle_tap(y2[:, j - 2, :], y1[:, j - 2, :], AXIS_W, j - 2)
-            if is_block(j - 4):
-                middle_tap(y3[:, j - 4, :], y2[:, j - 4, :], AXIS_H, j - 4)
-            if is_group_start(j - GROUP_LAG):
-                g = (j - GROUP_LAG) // PACK
+        for j in range(BLOCKS // PER_ROUND + 7):
+            for i in blocks_of(j - 4):
+                middle_tap(y3[:, i, :], y2[:, i, :], AXIS_H, i)
+            for i in blocks_of(j - 2):
+                middle_tap(y2[:, i, :], y1[:, i, :], AXIS_W, i)
+            for i in blocks_of(j):
+                g, t = divmod(i, PACK)
+                middle_tap(y1[:, i, :], turned[g][0][:, t, :], AXIS_D, i)
+            g = group_ending(j - 6)
+            if g is not None:
                 nc.scalar.copy(
                     out=y3_grouped[:, g],
                     in_=y3[:, PACK * g : PACK * (g + 1), :].rearrange("p t n -> p n t"),
                 )
             for k in (0, 2):
-                if is_block(j - 1):
-                    g, t = divmod(j - 1, PACK)
-                    outer_tap(y1[:, j - 1, :], turned[g][1 + k // 2][:, t, :], AXIS_D, k, j - 1)
-                if is_block(j - 3):
-                    outer_tap_in_sbuf(y2, y1, AXIS_W, k, j - 3, D, W)
-                if is_block(j - 5):
-                    outer_tap_in_sbuf(y3, y2, AXIS_H, k, j - 5, W * D, H)
-            if is_group_start(j - QUANTISE_LAG):
-                g = (j - QUANTISE_LAG) // PACK
+                for i in blocks_of(j - 5):
+                    outer_tap_in_sbuf(y3, y2, AXIS_H, k, i, W * D, H)
+                for i in blocks_of(j - 3):
+                    outer_tap_in_sbuf(y2, y1, AXIS_W, k, i, D, W)
+                for i in blocks_of(j - 1):
+                    g, t = divmod(i, PACK)
+                    outer_tap(y1[:, i, :], turned[g][1 + k // 2][:, t, :], AXIS_D, k, i)
+            g = group_ending(j - 7)
+            if g is not None:
                 nc.vector.quantize_mx(
                     out=y3_words[:, g, :].bitcast(FP8X4),
                     scales=y3_scales[:, g, :],
                     in_=y3_grouped[:, g].rearrange("p n t -> p (n t)"),
                 )
-            if is_group_start(j) and j // PACK + 1 < GROUPS:
-                turned.append(ranks_of_group(j // PACK + 1))
+            if j % ROUNDS_PER_GROUP == 0 and j // ROUNDS_PER_GROUP + 1 < GROUPS:
+                turned.append(ranks_of_group(j // ROUNDS_PER_GROUP + 1))
 
         out_sums = [banks.tile([P, K_PASS], F32, name="out_sum%d" % b, tag="bank") for b in range(GROUPS)]
         for g in range(GROUPS):

@@ -21,7 +21,9 @@ CHANNELS = 2048
 GROUPS = CHANNELS // K_PASS
 BLOCKS = CHANNELS // P
 PER_ROUND = 2
-ROUNDS_PER_GROUP = PACK // PER_ROUND
+ENTRY_ROUNDS = PACK // PER_ROUND
+ENTRY_PERIOD = 4
+TURN_ROUND = 2
 H, W, D = 8, 4, 4
 POS = H * W * D
 TAPS = 3
@@ -64,14 +66,25 @@ def tile_lowrankconv3d_w_kernel(
         nc.vector.memset(out_planes[:].bitcast(I32), 0)
 
         load_scale_planes(nc, in_planes, U_c_in_scales)
+        in_words = U_c_in_words.rearrange("k p n t -> p k (n t)")
         w_in = []
         for g in range(GROUPS):
             w_in.append(keep.tile([P, GROUPS, K_PASS], I32, name="w_in%d" % g, align_bytes=64))
-            for k in range(GROUPS):
-                words = U_c_in_words[k].rearrange("p n t -> p (n t)")
+            for k in range(0, GROUPS, 2):
                 nc.sync.dma_start(
-                    out=w_in[g][:, k, :],
-                    in_=words[:, PACK * K_PASS * g : PACK * K_PASS * (g + 1)].bitcast(I32),
+                    out=w_in[g][:, k : k + 2, :],
+                    in_=in_words[:, k : k + 2, PACK * K_PASS * g : PACK * K_PASS * (g + 1)].bitcast(I32),
+                )
+            if g == 0:
+                for axis, taps in enumerate((U_kh, U_kw, U_kd)):
+                    first = axis * TAPS * GROUPS
+                    nc.sync.dma_start(
+                        out=vectors[first : first + TAPS * GROUPS, :],
+                        in_=taps.rearrange("k (g c) -> (k g) c", g=GROUPS),
+                    )
+                nc.sync.dma_start(
+                    out=vectors[BIAS_ROW:VECTOR_ROWS, :],
+                    in_=bias.rearrange("(g c) -> g c", g=GROUPS),
                 )
         load_scale_planes(nc, out_planes, U_c_out_scales)
         w_out = []
@@ -80,16 +93,6 @@ def tile_lowrankconv3d_w_kernel(
             nc.sync.dma_start(
                 out=w_out[g][:], in_=U_c_out_words[g].rearrange("p n t -> p (n t)").bitcast(I32)
             )
-
-        for axis, taps in enumerate((U_kh, U_kw, U_kd)):
-            first = axis * TAPS * GROUPS
-            nc.scalar.dma_start(
-                out=vectors[first : first + TAPS * GROUPS, :],
-                in_=taps.rearrange("k (g c) -> (k g) c", g=GROUPS),
-            )
-        nc.scalar.dma_start(
-            out=vectors[BIAS_ROW:VECTOR_ROWS, :], in_=bias.rearrange("(g c) -> g c", g=GROUPS)
-        )
 
         ident_bf = keep.tile([P, P], BF16)
         make_identity(nc, ident_bf[:])
@@ -107,11 +110,7 @@ def tile_lowrankconv3d_w_kernel(
             out=from_above[:].rearrange("i (e d) -> i e d", d=D)[:, :, 0 : D - 1], in_=ident_d[:, :, 1:D]
         )
 
-        vectors_turned = banks.tile([P, PACK, P], BF16, tag="bank")
-        for t in range(PACK):
-            nc.tensor.transpose(vectors_turned[:, t, :], vectors[:, t:K_PASS:PACK], ident_bf[:])
         per_rank = keep.tile([P, PACK, VECTOR_ROWS], F32)
-        nc.scalar.activation(out=per_rank[:], in_=vectors_turned[:, :, 0:VECTOR_ROWS], func=COPY)
 
         def tap(axis, k, g, t):
             row = (axis * TAPS + k) * GROUPS + g
@@ -140,7 +139,7 @@ def tile_lowrankconv3d_w_kernel(
             copy(out=by_byte[:], in_=bank[:].rearrange("n (p t) -> n t p", t=PACK))
             return by_byte
 
-        def ranks_of_group(g):
+        def first_product(g):
             y0 = banks.tile([P, K_PASS], F32, tag="bank")
             for k in range(GROUPS):
                 nc.tensor.matmul_mx(
@@ -152,7 +151,9 @@ def tile_lowrankconv3d_w_kernel(
                     start=(k == 0),
                     stop=(k == GROUPS - 1),
                 )
-            by_byte = sort_by_byte(nc.scalar.copy, y0)
+            return y0
+
+        def turn_three_ways(by_byte):
             three_banks = []
             for matrix in (ident, from_below, from_above):
                 bank = banks.tile([P, PACK, POS], F32, tag="bank")
@@ -165,7 +166,15 @@ def tile_lowrankconv3d_w_kernel(
         y2 = keep.tile([P, BLOCKS, POS], F32)
         y3 = keep.tile([P, BLOCKS, POS], F32)
         y3_grouped = keep.tile([P, GROUPS, POS, PACK], BF16, align_bytes=64)
-        turned = [ranks_of_group(0)]
+
+        y0 = first_product(0)
+        vectors_turned = banks.tile([P, PACK, P], BF16, tag="bank")
+        for t in range(PACK):
+            nc.tensor.transpose(vectors_turned[:, t, :], vectors[:, t:K_PASS:PACK], ident_bf[:])
+        by_byte = sort_by_byte(nc.scalar.copy, y0)
+        nc.scalar.activation(out=per_rank[:], in_=vectors_turned[:, :, 0:VECTOR_ROWS], func=COPY)
+        turned = [turn_three_ways(by_byte)]
+        products = [first_product(1), first_product(2)]
 
         def middle_tap(dst, src, axis, i):
             g, t = divmod(i, PACK)
@@ -187,14 +196,17 @@ def tile_lowrankconv3d_w_kernel(
                 outer_tap(to[:, :, 0 : run - step], frm[:, :, step:run], axis, k, i)
 
         def blocks_of(entry_round):
-            first = entry_round * PER_ROUND
-            return [i for i in range(first, first + PER_ROUND) if 0 <= i < BLOCKS]
+            g, r = divmod(entry_round, ENTRY_PERIOD)
+            if not (0 <= g < GROUPS and r < ENTRY_ROUNDS):
+                return []
+            first = PACK * g + PER_ROUND * r
+            return list(range(first, first + PER_ROUND))
 
         def group_ending(entry_round):
-            g, rest = divmod(entry_round + 1, ROUNDS_PER_GROUP)
-            return g - 1 if rest == 0 and 1 <= g <= GROUPS else None
+            g, r = divmod(entry_round, ENTRY_PERIOD)
+            return g if 0 <= g < GROUPS and r == ENTRY_ROUNDS - 1 else None
 
-        for j in range(BLOCKS // PER_ROUND + 7):
+        for j in range(ENTRY_PERIOD * (GROUPS - 1) + ENTRY_ROUNDS + 7):
             for i in blocks_of(j - 4):
                 middle_tap(y3[:, i, :], y2[:, i, :], AXIS_H, i)
             for i in blocks_of(j - 2):
@@ -223,8 +235,11 @@ def tile_lowrankconv3d_w_kernel(
                     scales=y3_scales[:, g, :],
                     in_=y3_grouped[:, g].rearrange("p n t -> p (n t)"),
                 )
-            if j % ROUNDS_PER_GROUP == 0 and j // ROUNDS_PER_GROUP + 1 < GROUPS:
-                turned.append(ranks_of_group(j // ROUNDS_PER_GROUP + 1))
+            g, r = divmod(j, ENTRY_PERIOD)
+            if r == TURN_ROUND and g + 1 < GROUPS:
+                turned.append(turn_three_ways(sort_by_byte(nc.scalar.copy, products[g])))
+                if g + 3 < GROUPS:
+                    products.append(first_product(g + 3))
 
         out_sums = [banks.tile([P, K_PASS], F32, name="out_sum%d" % b, tag="bank") for b in range(GROUPS)]
         for g in range(GROUPS):

@@ -28,8 +28,9 @@ H, W, D = 8, 4, 4
 POS = H * W * D
 TAPS = 3
 AXIS_H, AXIS_W, AXIS_D = 0, 1, 2
-BIAS_ROW = 3 * TAPS * GROUPS
-VECTOR_ROWS = BIAS_ROW + GROUPS
+TAP_ROWS = 3 * TAPS * GROUPS
+PER_BANK = K_PASS // POS
+EARLY_PASSES = (3, 3, 2, 2)
 
 FLOPS = 2 * 2 * POS * CHANNELS * CHANNELS + 2 * 3 * TAPS * POS * CHANNELS
 
@@ -60,6 +61,8 @@ def tile_lowrankconv3d_w_kernel(
 
         vectors = keep.tile([P, K_PASS], BF16)
         nc.vector.memset(vectors[:], 0.0)
+        bias_rows = keep.tile([P, P], BF16)
+        nc.vector.memset(bias_rows[:], 0.0)
         in_planes = keep.tile([P, CHANNELS], U8, align_bytes=64)
         out_planes = keep.tile([P, CHANNELS], U8, align_bytes=64)
         nc.vector.memset(in_planes[:].bitcast(I32), 0)
@@ -82,10 +85,7 @@ def tile_lowrankconv3d_w_kernel(
                         out=vectors[first : first + TAPS * GROUPS, :],
                         in_=taps.rearrange("k (g c) -> (k g) c", g=GROUPS),
                     )
-                nc.sync.dma_start(
-                    out=vectors[BIAS_ROW:VECTOR_ROWS, :],
-                    in_=bias.rearrange("(g c) -> g c", g=GROUPS),
-                )
+                nc.sync.dma_start(out=bias_rows[0:BLOCKS, :], in_=bias.rearrange("(b c) -> b c", b=BLOCKS))
         load_scale_planes(nc, out_planes, U_c_out_scales)
         w_out = []
         for g in range(GROUPS):
@@ -110,7 +110,8 @@ def tile_lowrankconv3d_w_kernel(
             out=from_above[:].rearrange("i (e d) -> i e d", d=D)[:, :, 0 : D - 1], in_=ident_d[:, :, 1:D]
         )
 
-        per_rank = keep.tile([P, PACK, VECTOR_ROWS], F32)
+        per_rank = keep.tile([P, PACK, TAP_ROWS], F32)
+        per_channel = keep.tile([P, BLOCKS], F32)
 
         def tap(axis, k, g, t):
             row = (axis * TAPS + k) * GROUPS + g
@@ -168,11 +169,13 @@ def tile_lowrankconv3d_w_kernel(
         y3_grouped = keep.tile([P, GROUPS, POS, PACK], BF16, align_bytes=64)
 
         y0 = first_product(0)
-        vectors_turned = banks.tile([P, PACK, P], BF16, tag="bank")
+        vectors_turned = banks.tile([P, PACK + 1, P], BF16, tag="bank")
         for t in range(PACK):
             nc.tensor.transpose(vectors_turned[:, t, :], vectors[:, t:K_PASS:PACK], ident_bf[:])
+        nc.tensor.transpose(vectors_turned[:, PACK, :], bias_rows[:], ident_bf[:])
         by_byte = sort_by_byte(nc.scalar.copy, y0)
-        nc.scalar.activation(out=per_rank[:], in_=vectors_turned[:, :, 0:VECTOR_ROWS], func=COPY)
+        nc.scalar.activation(out=per_rank[:], in_=vectors_turned[:, 0:PACK, 0:TAP_ROWS], func=COPY)
+        nc.vector.tensor_copy(out=per_channel[:], in_=vectors_turned[:, PACK, 0:BLOCKS])
         turned = [turn_three_ways(by_byte)]
         products = [first_product(1), first_product(2)]
 
@@ -206,6 +209,35 @@ def tile_lowrankconv3d_w_kernel(
             g, r = divmod(entry_round, ENTRY_PERIOD)
             return g if 0 <= g < GROUPS and r == ENTRY_ROUNDS - 1 else None
 
+        early = keep.tile([P, GROUPS, PER_BANK, POS], F32)
+
+        def channel_bank(q, passes):
+            bank = banks.tile([P, PER_BANK, POS], F32, tag="bank")
+            for j in range(PER_BANK):
+                first = P * (PER_BANK * q + j)
+                for g in passes:
+                    nc.tensor.matmul_mx(
+                        out=bank[:, j, :],
+                        lhsT=w_out[g][:, first : first + P].bitcast(FP8X4),
+                        lhsT_scale=out_planes[PACK * g : P, first : first + P],
+                        rhs=y3_words[:, g, :].bitcast(FP8X4),
+                        rhs_scale=y3_scales[:, g, :],
+                        start=(g == passes[0]),
+                        stop=(g == passes[-1]),
+                    )
+            return bank
+
+        def add_bias(q, bank):
+            for j in range(PER_BANK):
+                b = PER_BANK * q + j
+                nc.scalar.activation(
+                    out=early[:, q, j, :], in_=bank[:, j, :], func=IDENTITY, bias=per_channel[:, b : b + 1]
+                )
+
+        early_banks = []
+        emptied = 0
+        copied = 0
+
         for j in range(ENTRY_PERIOD * (GROUPS - 1) + ENTRY_ROUNDS + 7):
             for i in blocks_of(j - 4):
                 middle_tap(y3[:, i, :], y2[:, i, :], AXIS_H, i)
@@ -220,6 +252,10 @@ def tile_lowrankconv3d_w_kernel(
                     out=y3_grouped[:, g],
                     in_=y3[:, PACK * g : PACK * (g + 1), :].rearrange("p t n -> p n t"),
                 )
+                copied = g + 1
+            if emptied < len(early_banks) and copied > EARLY_PASSES[early_banks[emptied][0]]:
+                add_bias(*early_banks[emptied])
+                emptied += 1
             for k in (0, 2):
                 for i in blocks_of(j - 5):
                     outer_tap_in_sbuf(y3, y2, AXIS_H, k, i, W * D, H)
@@ -235,46 +271,18 @@ def tile_lowrankconv3d_w_kernel(
                     scales=y3_scales[:, g, :],
                     in_=y3_grouped[:, g].rearrange("p n t -> p (n t)"),
                 )
+                for q in range(GROUPS):
+                    if EARLY_PASSES[q] == g + 1:
+                        early_banks.append((q, channel_bank(q, range(g + 1))))
             g, r = divmod(j, ENTRY_PERIOD)
             if r == TURN_ROUND and g + 1 < GROUPS:
                 turned.append(turn_three_ways(sort_by_byte(nc.scalar.copy, products[g])))
                 if g + 3 < GROUPS:
                     products.append(first_product(g + 3))
 
-        out_sums = [banks.tile([P, K_PASS], F32, name="out_sum%d" % b, tag="bank") for b in range(GROUPS)]
-        for g in range(GROUPS):
-            for b in range(GROUPS):
-                nc.tensor.matmul_mx(
-                    out=out_sums[b][:],
-                    lhsT=y3_words[:, g, :].bitcast(FP8X4),
-                    lhsT_scale=y3_scales[:, g, :],
-                    rhs=w_out[g][:, K_PASS * b : K_PASS * (b + 1)].bitcast(FP8X4),
-                    rhs_scale=out_planes[PACK * g : P, K_PASS * b : K_PASS * (b + 1)],
-                    start=(g == 0),
-                    stop=(g == GROUPS - 1),
-                )
-
-        out_blocks = out.rearrange("a (b p t) h w d -> b p (a t h w d)", p=P, t=PACK)
-        for b in range(GROUPS):
-            on_scalar = b % 2 == 0
-            by_byte = sort_by_byte(nc.scalar.copy if on_scalar else nc.vector.tensor_copy, out_sums[b])
-            bank = banks.tile([P, PACK, POS], F32, tag="bank")
-            for t in range(PACK):
-                nc.tensor.transpose(bank[:, t, :], by_byte[:, t, :], ident[:])
-            result = results.tile([P, PACK, POS], F32)
-            if on_scalar:
-                for t in range(PACK):
-                    nc.scalar.activation(
-                        out=result[:, t, :],
-                        in_=bank[:, t, :],
-                        func=IDENTITY,
-                        bias=per_rank[:, t, BIAS_ROW + b : BIAS_ROW + b + 1],
-                    )
-            else:
-                nc.vector.tensor_tensor(
-                    out=result[:],
-                    in0=bank[:],
-                    in1=per_rank[:, :, BIAS_ROW + b : BIAS_ROW + b + 1].to_broadcast([P, PACK, POS]),
-                    op=ADD,
-                )
-            nc.sync.dma_start(out=out_blocks[b], in_=result[:].rearrange("p t n -> p (t n)"))
+        out_banks = out.rearrange("a (q j p) h w d -> q p j (a h w d)", p=P, j=PER_BANK)
+        for q in range(GROUPS):
+            rest = channel_bank(q, range(EARLY_PASSES[q], GROUPS))
+            result = results.tile([P, PER_BANK, POS], F32)
+            nc.vector.tensor_tensor(out=result[:], in0=rest[:], in1=early[:, q], op=ADD)
+            nc.sync.dma_start(out=out_banks[q], in_=result[:])

@@ -28,7 +28,11 @@ H, W, D = 8, 4, 4
 POS = H * W * D
 TAPS = 3
 AXIS_H, AXIS_W, AXIS_D = 0, 1, 2
-TAP_ROWS = 3 * TAPS * GROUPS
+AXIS_ROWS = TAPS * GROUPS
+TENSOR_GROUPS = (0,)
+TENSOR_ROUNDS = (5, 8, 11, 12)
+TENSOR_COPY_ROUND = 14
+EDGE = W * D
 PER_BANK = K_PASS // POS
 EARLY_PASSES = (3, 3, 2, 2)
 
@@ -59,33 +63,41 @@ def tile_lowrankconv3d_w_kernel(
             out=x_raw[:], in_=x.rearrange("b (g p t) h w d -> p (b g) t (h w d)", p=P, t=PACK)
         )
 
+        vectors_h = keep.tile([P, K_PASS], BF16)
         vectors = keep.tile([P, K_PASS], BF16)
-        nc.vector.memset(vectors[:], 0.0)
+        nc.vector.memset(vectors_h[:], 0.0)
         bias_rows = keep.tile([P, P], BF16)
         nc.vector.memset(bias_rows[:], 0.0)
+        loaded = keep.tile([P, 1], F32)
+        nc.scalar.activation(out=loaded[:], in_=bias_rows[:, 0:1], func=COPY)
         in_planes = keep.tile([P, CHANNELS], U8, align_bytes=64)
         out_planes = keep.tile([P, CHANNELS], U8, align_bytes=64)
         nc.vector.memset(in_planes[:].bitcast(I32), 0)
+        nc.vector.memset(vectors[:], 0.0)
         nc.vector.memset(out_planes[:].bitcast(I32), 0)
+        y2 = keep.tile([P, BLOCKS, EDGE + POS + EDGE], F32)
+        nc.vector.memset(y2[:, :, 0:EDGE], 0.0)
+        nc.vector.memset(y2[:, :, EDGE + POS :], 0.0)
 
+        nc.scalar.dma_start(
+            out=vectors_h[0:AXIS_ROWS, :], in_=U_kh.rearrange("k (g c) -> (k g) c", g=GROUPS)
+        )
         load_scale_planes(nc, in_planes, U_c_in_scales)
         in_words = U_c_in_words.rearrange("k p n t -> p k (n t)")
         w_in = []
         for g in range(GROUPS):
             w_in.append(keep.tile([P, GROUPS, K_PASS], I32, name="w_in%d" % g, align_bytes=64))
-            for k in range(0, GROUPS, 2):
+            for first, end in ((0, 1), (1, 2), (2, 4)) if g == 0 else ((0, 2), (2, 4)):
                 nc.sync.dma_start(
-                    out=w_in[g][:, k : k + 2, :],
-                    in_=in_words[:, k : k + 2, PACK * K_PASS * g : PACK * K_PASS * (g + 1)].bitcast(I32),
+                    out=w_in[g][:, first:end, :],
+                    in_=in_words[:, first:end, PACK * K_PASS * g : PACK * K_PASS * (g + 1)].bitcast(I32),
                 )
             if g == 0:
-                for axis, taps in enumerate((U_kh, U_kw, U_kd)):
-                    first = axis * TAPS * GROUPS
+                for n, taps in enumerate((U_kw, U_kd)):
                     nc.sync.dma_start(
-                        out=vectors[first : first + TAPS * GROUPS, :],
+                        out=vectors[AXIS_ROWS * n : AXIS_ROWS * (n + 1), :],
                         in_=taps.rearrange("k (g c) -> (k g) c", g=GROUPS),
                     )
-                nc.sync.dma_start(out=bias_rows[0:BLOCKS, :], in_=bias.rearrange("(b c) -> b c", b=BLOCKS))
         load_scale_planes(nc, out_planes, U_c_out_scales)
         w_out = []
         for g in range(GROUPS):
@@ -98,6 +110,7 @@ def tile_lowrankconv3d_w_kernel(
         make_identity(nc, ident_bf[:])
         ident = keep.tile([P, P], F32)
         make_identity(nc, ident[:])
+        nc.gpsimd.dma_start(out=bias_rows[0:BLOCKS, :], in_=bias.rearrange("(b c) -> b c", b=BLOCKS))
         from_below = keep.tile([P, POS], F32)
         from_above = keep.tile([P, POS], F32)
         nc.vector.memset(from_below[:], 0.0)
@@ -110,12 +123,16 @@ def tile_lowrankconv3d_w_kernel(
             out=from_above[:].rearrange("i (e d) -> i e d", d=D)[:, :, 0 : D - 1], in_=ident_d[:, :, 1:D]
         )
 
-        per_rank = keep.tile([P, PACK, TAP_ROWS], F32)
+        taps_h = keep.tile([P, PACK, AXIS_ROWS], F32)
+        taps_wd = keep.tile([P, PACK, 2 * AXIS_ROWS], F32)
         per_channel = keep.tile([P, BLOCKS], F32)
 
         def tap(axis, k, g, t):
-            row = (axis * TAPS + k) * GROUPS + g
-            return per_rank[:, t, row : row + 1]
+            if axis == AXIS_H:
+                row = k * GROUPS + g
+                return taps_h[:, t, row : row + 1]
+            row = ((axis - AXIS_W) * TAPS + k) * GROUPS + g
+            return taps_wd[:, t, row : row + 1]
 
         x_grouped = keep.tile([P, GROUPS, POS, PACK], BF16, align_bytes=64)
         x_words = keep.tile([P, GROUPS, POS], U32, align_bytes=64)
@@ -155,18 +172,31 @@ def tile_lowrankconv3d_w_kernel(
             return y0
 
         def turn_three_ways(by_byte):
-            three_banks = []
-            for matrix in (ident, from_below, from_above):
-                bank = banks.tile([P, PACK, POS], F32, tag="bank")
-                for t in range(PACK):
-                    nc.tensor.transpose(bank[:, t, :], by_byte[:, t, :], matrix[:])
-                three_banks.append(bank)
-            return three_banks
+            plain = banks.tile([P, PACK, POS], F32, tag="bank")
+            for t in range(PACK):
+                nc.tensor.transpose(plain[:, t, :], by_byte[:, t, :], ident[:])
+            shifted = []
+            for first in range(0, PACK, PER_ROUND):
+                bank = banks.tile([P, PER_ROUND, 2, POS], F32, tag="bank")
+                for t in range(PER_ROUND):
+                    for way, matrix in enumerate((from_below, from_above)):
+                        nc.tensor.transpose(bank[:, t, way, :], by_byte[:, first + t, :], matrix[:])
+                shifted.append(bank)
+            return plain, shifted
 
         y1 = keep.tile([P, BLOCKS, POS], F32)
-        y2 = keep.tile([P, BLOCKS, POS], F32)
         y3 = keep.tile([P, BLOCKS, POS], F32)
         y3_grouped = keep.tile([P, GROUPS, POS, PACK], BF16, align_bytes=64)
+
+        vectors_turned = banks.tile([P, PACK, P], BF16, tag="bank")
+        for t in range(PACK):
+            nc.tensor.transpose(vectors_turned[:, t, :], vectors_h[:, t:K_PASS:PACK], ident_bf[:])
+        nc.vector.tensor_copy(out=taps_h[:], in_=vectors_turned[:, :, 0:AXIS_ROWS])
+        diagonal = keep.tile([P, len(TENSOR_GROUPS), PACK, TAPS, P], F32)
+        for n, g in enumerate(TENSOR_GROUPS):
+            for t in range(PACK):
+                for k in range(TAPS):
+                    nc.vector.tensor_scalar_mul(diagonal[:, n, t, k, :], ident[:], tap(AXIS_H, k, g, t))
 
         y0 = first_product(0)
         vectors_turned = banks.tile([P, PACK + 1, P], BF16, tag="bank")
@@ -174,10 +204,10 @@ def tile_lowrankconv3d_w_kernel(
             nc.tensor.transpose(vectors_turned[:, t, :], vectors[:, t:K_PASS:PACK], ident_bf[:])
         nc.tensor.transpose(vectors_turned[:, PACK, :], bias_rows[:], ident_bf[:])
         by_byte = sort_by_byte(nc.scalar.copy, y0)
-        nc.scalar.activation(out=per_rank[:], in_=vectors_turned[:, 0:PACK, 0:TAP_ROWS], func=COPY)
+        nc.scalar.activation(out=taps_wd[:], in_=vectors_turned[:, 0:PACK, 0 : 2 * AXIS_ROWS], func=COPY)
         nc.vector.tensor_copy(out=per_channel[:], in_=vectors_turned[:, PACK, 0:BLOCKS])
         turned = [turn_three_ways(by_byte)]
-        products = [first_product(1), first_product(2)]
+        products = [first_product(1)]
 
         def middle_tap(dst, src, axis, i):
             g, t = divmod(i, PACK)
@@ -197,6 +227,29 @@ def tile_lowrankconv3d_w_kernel(
                 outer_tap(to[:, :, step:run], frm[:, :, 0 : run - step], axis, k, i)
             else:
                 outer_tap(to[:, :, 0 : run - step], frm[:, :, step:run], axis, k, i)
+
+        y2_inner = y2[:, :, EDGE : EDGE + POS]
+
+        def filter_h_on_tensor(bank, g, t):
+            for k in range(TAPS):
+                first = EDGE * k
+                nc.tensor.matmul(
+                    bank[:, t, :],
+                    lhsT=diagonal[:, TENSOR_GROUPS.index(g), t, k, :],
+                    rhs=y2[:, PACK * g + t, first : first + POS],
+                    start=(k == 0),
+                    stop=(k == TAPS - 1),
+                )
+
+        def group_to_copy(j):
+            for g in range(GROUPS):
+                rounds = TENSOR_COPY_ROUND if g in TENSOR_GROUPS else ENTRY_ROUNDS - 1 + 6
+                if j == ENTRY_PERIOD * g + rounds:
+                    return g
+            return None
+
+        def h_blocks(entry_round):
+            return [i for i in blocks_of(entry_round) if i // PACK not in TENSOR_GROUPS]
 
         def blocks_of(entry_round):
             g, r = divmod(entry_round, ENTRY_PERIOD)
@@ -235,50 +288,69 @@ def tile_lowrankconv3d_w_kernel(
                 )
 
         early_banks = []
-        emptied = 0
-        copied = 0
+        quantised = set()
+        filtered = {}
 
-        for j in range(ENTRY_PERIOD * (GROUPS - 1) + ENTRY_ROUNDS + 7):
-            for i in blocks_of(j - 4):
-                middle_tap(y3[:, i, :], y2[:, i, :], AXIS_H, i)
+        for j in range(ENTRY_PERIOD * (GROUPS - 1) + ENTRY_ROUNDS + 5):
+            for i in h_blocks(j - 4):
+                middle_tap(y3[:, i, :], y2_inner[:, i, :], AXIS_H, i)
             for i in blocks_of(j - 2):
-                middle_tap(y2[:, i, :], y1[:, i, :], AXIS_W, i)
+                middle_tap(y2_inner[:, i, :], y1[:, i, :], AXIS_W, i)
             for i in blocks_of(j):
                 g, t = divmod(i, PACK)
                 middle_tap(y1[:, i, :], turned[g][0][:, t, :], AXIS_D, i)
-            g = group_ending(j - 6)
-            if g is not None:
-                nc.scalar.copy(
-                    out=y3_grouped[:, g],
-                    in_=y3[:, PACK * g : PACK * (g + 1), :].rearrange("p t n -> p n t"),
-                )
-                copied = g + 1
-            if emptied < len(early_banks) and copied > EARLY_PASSES[early_banks[emptied][0]]:
-                add_bias(*early_banks[emptied])
-                emptied += 1
+            g = group_to_copy(j)
+            if g is not None and g < GROUPS - 1:
+                whole = filtered[g][:] if g in TENSOR_GROUPS else y3[:, PACK * g : PACK * (g + 1), :]
+                nc.scalar.copy(out=y3_grouped[:, g], in_=whole.rearrange("p t n -> p n t"))
             for k in (0, 2):
-                for i in blocks_of(j - 5):
-                    outer_tap_in_sbuf(y3, y2, AXIS_H, k, i, W * D, H)
+                for i in h_blocks(j - 5):
+                    outer_tap_in_sbuf(y3, y2_inner, AXIS_H, k, i, W * D, H)
                 for i in blocks_of(j - 3):
-                    outer_tap_in_sbuf(y2, y1, AXIS_W, k, i, D, W)
+                    outer_tap_in_sbuf(y2_inner, y1, AXIS_W, k, i, D, W)
                 for i in blocks_of(j - 1):
                     g, t = divmod(i, PACK)
-                    outer_tap(y1[:, i, :], turned[g][1 + k // 2][:, t, :], AXIS_D, k, i)
-            g = group_ending(j - 7)
-            if g is not None:
+                    block, place = divmod(t, PER_ROUND)
+                    outer_tap(y1[:, i, :], turned[g][1][block][:, place, k // 2, :], AXIS_D, k, i)
+            for g in TENSOR_GROUPS:
+                age = j - ENTRY_PERIOD * g
+                if age in TENSOR_ROUNDS:
+                    if g not in filtered:
+                        filtered[g] = banks.tile([P, PACK, POS], F32, name="filtered%d" % g, tag="bank")
+                    filter_h_on_tensor(filtered[g], g, TENSOR_ROUNDS.index(age))
+            g = group_to_copy(j - 1)
+            if g is not None and g < GROUPS - 1:
                 nc.vector.quantize_mx(
                     out=y3_words[:, g, :].bitcast(FP8X4),
                     scales=y3_scales[:, g, :],
                     in_=y3_grouped[:, g].rearrange("p n t -> p (n t)"),
                 )
+                quantised.add(g)
                 for q in range(GROUPS):
-                    if EARLY_PASSES[q] == g + 1:
-                        early_banks.append((q, channel_bank(q, range(g + 1))))
+                    passes = range(EARLY_PASSES[q])
+                    if g in passes and all(n in quantised for n in passes):
+                        early_banks.append((q, channel_bank(q, passes)))
             g, r = divmod(j, ENTRY_PERIOD)
             if r == TURN_ROUND and g + 1 < GROUPS:
                 turned.append(turn_three_ways(sort_by_byte(nc.scalar.copy, products[g])))
-                if g + 3 < GROUPS:
-                    products.append(first_product(g + 3))
+                if g + 2 < GROUPS:
+                    products.append(first_product(g + 2))
+
+        last = GROUPS - 1
+        halves = [slice(0, POS // 2), slice(POS // 2, POS)]
+        for half in halves:
+            nc.vector.tensor_copy(
+                out=y3_grouped[:, last, half],
+                in_=y3[:, PACK * last : PACK * GROUPS, half].rearrange("p t n -> p n t"),
+            )
+        for half in halves:
+            nc.vector.quantize_mx(
+                out=y3_words[:, last, half].bitcast(FP8X4),
+                scales=y3_scales[:, last, half],
+                in_=y3_grouped[:, last, half].rearrange("p n t -> p (n t)"),
+            )
+        for q, bank in early_banks:
+            add_bias(q, bank)
 
         out_banks = out.rearrange("a (q j p) h w d -> q p j (a h w d)", p=P, j=PER_BANK)
         for q in range(GROUPS):

@@ -29,10 +29,6 @@ POS = H * W * D
 TAPS = 3
 AXIS_H, AXIS_W, AXIS_D = 0, 1, 2
 AXIS_ROWS = TAPS * GROUPS
-TENSOR_GROUPS = (0,)
-TENSOR_ROUNDS = (5, 8, 11, 12)
-TENSOR_COPY_ROUND = 14
-EDGE = W * D
 PER_BANK = K_PASS // POS
 EARLY_PASSES = (3, 3, 2, 2)
 
@@ -75,9 +71,7 @@ def tile_lowrankconv3d_w_kernel(
         nc.vector.memset(in_planes[:].bitcast(I32), 0)
         nc.vector.memset(vectors[:], 0.0)
         nc.vector.memset(out_planes[:].bitcast(I32), 0)
-        y2 = keep.tile([P, BLOCKS, EDGE + POS + EDGE], F32)
-        nc.vector.memset(y2[:, :, 0:EDGE], 0.0)
-        nc.vector.memset(y2[:, :, EDGE + POS :], 0.0)
+        y2 = keep.tile([P, BLOCKS, POS], F32)
 
         nc.scalar.dma_start(
             out=vectors_h[0:AXIS_ROWS, :], in_=U_kh.rearrange("k (g c) -> (k g) c", g=GROUPS)
@@ -192,11 +186,6 @@ def tile_lowrankconv3d_w_kernel(
         for t in range(PACK):
             nc.tensor.transpose(vectors_turned[:, t, :], vectors_h[:, t:K_PASS:PACK], ident_bf[:])
         nc.vector.tensor_copy(out=taps_h[:], in_=vectors_turned[:, :, 0:AXIS_ROWS])
-        diagonal = keep.tile([P, len(TENSOR_GROUPS), PACK, TAPS, P], F32)
-        for n, g in enumerate(TENSOR_GROUPS):
-            for t in range(PACK):
-                for k in range(TAPS):
-                    nc.vector.tensor_scalar_mul(diagonal[:, n, t, k, :], ident[:], tap(AXIS_H, k, g, t))
 
         y0 = first_product(0)
         vectors_turned = banks.tile([P, PACK + 1, P], BF16, tag="bank")
@@ -227,29 +216,6 @@ def tile_lowrankconv3d_w_kernel(
                 outer_tap(to[:, :, step:run], frm[:, :, 0 : run - step], axis, k, i)
             else:
                 outer_tap(to[:, :, 0 : run - step], frm[:, :, step:run], axis, k, i)
-
-        y2_inner = y2[:, :, EDGE : EDGE + POS]
-
-        def filter_h_on_tensor(bank, g, t):
-            for k in range(TAPS):
-                first = EDGE * k
-                nc.tensor.matmul(
-                    bank[:, t, :],
-                    lhsT=diagonal[:, TENSOR_GROUPS.index(g), t, k, :],
-                    rhs=y2[:, PACK * g + t, first : first + POS],
-                    start=(k == 0),
-                    stop=(k == TAPS - 1),
-                )
-
-        def group_to_copy(j):
-            for g in range(GROUPS):
-                rounds = TENSOR_COPY_ROUND if g in TENSOR_GROUPS else ENTRY_ROUNDS - 1 + 6
-                if j == ENTRY_PERIOD * g + rounds:
-                    return g
-            return None
-
-        def h_blocks(entry_round):
-            return [i for i in blocks_of(entry_round) if i // PACK not in TENSOR_GROUPS]
 
         def blocks_of(entry_round):
             g, r = divmod(entry_round, ENTRY_PERIOD)
@@ -289,36 +255,28 @@ def tile_lowrankconv3d_w_kernel(
 
         early_banks = []
         quantised = set()
-        filtered = {}
 
         for j in range(ENTRY_PERIOD * (GROUPS - 1) + ENTRY_ROUNDS + 5):
-            for i in h_blocks(j - 4):
-                middle_tap(y3[:, i, :], y2_inner[:, i, :], AXIS_H, i)
+            for i in blocks_of(j - 4):
+                middle_tap(y3[:, i, :], y2[:, i, :], AXIS_H, i)
             for i in blocks_of(j - 2):
-                middle_tap(y2_inner[:, i, :], y1[:, i, :], AXIS_W, i)
+                middle_tap(y2[:, i, :], y1[:, i, :], AXIS_W, i)
             for i in blocks_of(j):
                 g, t = divmod(i, PACK)
                 middle_tap(y1[:, i, :], turned[g][0][:, t, :], AXIS_D, i)
-            g = group_to_copy(j)
+            g = group_ending(j - 6)
             if g is not None and g < GROUPS - 1:
-                whole = filtered[g][:] if g in TENSOR_GROUPS else y3[:, PACK * g : PACK * (g + 1), :]
-                nc.scalar.copy(out=y3_grouped[:, g], in_=whole.rearrange("p t n -> p n t"))
+                nc.scalar.copy(out=y3_grouped[:, g], in_=y3[:, PACK * g : PACK * (g + 1), :].rearrange("p t n -> p n t"))
             for k in (0, 2):
-                for i in h_blocks(j - 5):
-                    outer_tap_in_sbuf(y3, y2_inner, AXIS_H, k, i, W * D, H)
+                for i in blocks_of(j - 5):
+                    outer_tap_in_sbuf(y3, y2, AXIS_H, k, i, W * D, H)
                 for i in blocks_of(j - 3):
-                    outer_tap_in_sbuf(y2_inner, y1, AXIS_W, k, i, D, W)
+                    outer_tap_in_sbuf(y2, y1, AXIS_W, k, i, D, W)
                 for i in blocks_of(j - 1):
                     g, t = divmod(i, PACK)
                     block, place = divmod(t, PER_ROUND)
                     outer_tap(y1[:, i, :], turned[g][1][block][:, place, k // 2, :], AXIS_D, k, i)
-            for g in TENSOR_GROUPS:
-                age = j - ENTRY_PERIOD * g
-                if age in TENSOR_ROUNDS:
-                    if g not in filtered:
-                        filtered[g] = banks.tile([P, PACK, POS], F32, name="filtered%d" % g, tag="bank")
-                    filter_h_on_tensor(filtered[g], g, TENSOR_ROUNDS.index(age))
-            g = group_to_copy(j - 1)
+            g = group_ending(j - 7)
             if g is not None and g < GROUPS - 1:
                 nc.vector.quantize_mx(
                     out=y3_words[:, g, :].bitcast(FP8X4),

@@ -59,9 +59,7 @@ def tile_lowrankconv3d_w_kernel(
             out=x_raw[:], in_=x.rearrange("b (g p t) h w d -> p (b g) t (h w d)", p=P, t=PACK)
         )
 
-        vectors_h = keep.tile([P, K_PASS], BF16)
         vectors = keep.tile([P, K_PASS], BF16)
-        nc.vector.memset(vectors_h[:], 0.0)
         bias_rows = keep.tile([P, P], BF16)
         nc.vector.memset(bias_rows[:], 0.0)
         loaded = keep.tile([P, 1], F32)
@@ -73,9 +71,6 @@ def tile_lowrankconv3d_w_kernel(
         nc.vector.memset(out_planes[:].bitcast(I32), 0)
         y2 = keep.tile([P, BLOCKS, POS], F32)
 
-        nc.scalar.dma_start(
-            out=vectors_h[0:AXIS_ROWS, :], in_=U_kh.rearrange("k (g c) -> (k g) c", g=GROUPS)
-        )
         load_scale_planes(nc, in_planes, U_c_in_scales)
         in_words = U_c_in_words.rearrange("k p n t -> p k (n t)")
         w_in = []
@@ -87,11 +82,14 @@ def tile_lowrankconv3d_w_kernel(
                     in_=in_words[:, first:end, PACK * K_PASS * g : PACK * K_PASS * (g + 1)].bitcast(I32),
                 )
             if g == 0:
-                for n, taps in enumerate((U_kw, U_kd)):
+                for n, taps in enumerate((U_kh, U_kw, U_kd)):
                     nc.sync.dma_start(
                         out=vectors[AXIS_ROWS * n : AXIS_ROWS * (n + 1), :],
                         in_=taps.rearrange("k (g c) -> (k g) c", g=GROUPS),
                     )
+                nc.sync.dma_start(
+                    out=bias_rows[0:BLOCKS, :], in_=bias.rearrange("(b c) -> b c", b=BLOCKS)
+                )
         load_scale_planes(nc, out_planes, U_c_out_scales)
         w_out = []
         for g in range(GROUPS):
@@ -104,7 +102,6 @@ def tile_lowrankconv3d_w_kernel(
         make_identity(nc, ident_bf[:])
         ident = keep.tile([P, P], F32)
         make_identity(nc, ident[:])
-        nc.gpsimd.dma_start(out=bias_rows[0:BLOCKS, :], in_=bias.rearrange("(b c) -> b c", b=BLOCKS))
         from_below = keep.tile([P, POS], F32)
         from_above = keep.tile([P, POS], F32)
         nc.vector.memset(from_below[:], 0.0)
@@ -117,16 +114,12 @@ def tile_lowrankconv3d_w_kernel(
             out=from_above[:].rearrange("i (e d) -> i e d", d=D)[:, :, 0 : D - 1], in_=ident_d[:, :, 1:D]
         )
 
-        taps_h = keep.tile([P, PACK, AXIS_ROWS], F32)
-        taps_wd = keep.tile([P, PACK, 2 * AXIS_ROWS], F32)
+        per_rank = keep.tile([P, PACK, 3 * AXIS_ROWS], F32)
         per_channel = keep.tile([P, BLOCKS], F32)
 
         def tap(axis, k, g, t):
-            if axis == AXIS_H:
-                row = k * GROUPS + g
-                return taps_h[:, t, row : row + 1]
-            row = ((axis - AXIS_W) * TAPS + k) * GROUPS + g
-            return taps_wd[:, t, row : row + 1]
+            row = (axis * TAPS + k) * GROUPS + g
+            return per_rank[:, t, row : row + 1]
 
         x_grouped = keep.tile([P, GROUPS, POS, PACK], BF16, align_bytes=64)
         x_words = keep.tile([P, GROUPS, POS], U32, align_bytes=64)
@@ -182,18 +175,13 @@ def tile_lowrankconv3d_w_kernel(
         y3 = keep.tile([P, BLOCKS, POS], F32)
         y3_grouped = keep.tile([P, GROUPS, POS, PACK], BF16, align_bytes=64)
 
-        vectors_turned = banks.tile([P, PACK, P], BF16, tag="bank")
-        for t in range(PACK):
-            nc.tensor.transpose(vectors_turned[:, t, :], vectors_h[:, t:K_PASS:PACK], ident_bf[:])
-        nc.vector.tensor_copy(out=taps_h[:], in_=vectors_turned[:, :, 0:AXIS_ROWS])
-
         y0 = first_product(0)
         vectors_turned = banks.tile([P, PACK + 1, P], BF16, tag="bank")
         for t in range(PACK):
             nc.tensor.transpose(vectors_turned[:, t, :], vectors[:, t:K_PASS:PACK], ident_bf[:])
         nc.tensor.transpose(vectors_turned[:, PACK, :], bias_rows[:], ident_bf[:])
         by_byte = sort_by_byte(nc.scalar.copy, y0)
-        nc.scalar.activation(out=taps_wd[:], in_=vectors_turned[:, 0:PACK, 0 : 2 * AXIS_ROWS], func=COPY)
+        nc.scalar.activation(out=per_rank[:], in_=vectors_turned[:, 0:PACK, 0 : 3 * AXIS_ROWS], func=COPY)
         nc.vector.tensor_copy(out=per_channel[:], in_=vectors_turned[:, PACK, 0:BLOCKS])
         turned = [turn_three_ways(by_byte)]
         products = [first_product(1)]

@@ -20,10 +20,7 @@ K_PASS = P * PACK
 CHANNELS = 2048
 GROUPS = CHANNELS // K_PASS
 BLOCKS = CHANNELS // P
-PER_ROUND = 2
-ENTRY_ROUNDS = PACK // PER_ROUND
-ENTRY_PERIOD = 4
-TURN_ROUND = 2
+AHEAD = 2
 H, W, D = 8, 4, 4
 POS = H * W * D
 TAPS = 3
@@ -159,17 +156,13 @@ def tile_lowrankconv3d_w_kernel(
             return y0
 
         def turn_three_ways(by_byte):
-            plain = banks.tile([P, PACK, POS], F32, tag="bank")
-            for t in range(PACK):
-                nc.tensor.transpose(plain[:, t, :], by_byte[:, t, :], ident[:])
-            shifted = []
-            for first in range(0, PACK, PER_ROUND):
-                bank = banks.tile([P, PER_ROUND, 2, POS], F32, tag="bank")
-                for t in range(PER_ROUND):
-                    for way, matrix in enumerate((from_below, from_above)):
-                        nc.tensor.transpose(bank[:, t, way, :], by_byte[:, first + t, :], matrix[:])
-                shifted.append(bank)
-            return plain, shifted
+            three_banks = []
+            for matrix in (ident, from_below, from_above):
+                bank = banks.tile([P, PACK, POS], F32, tag="bank")
+                for t in range(PACK):
+                    nc.tensor.transpose(bank[:, t, :], by_byte[:, t, :], matrix[:])
+                three_banks.append(bank)
+            return three_banks
 
         y1 = keep.tile([P, BLOCKS, POS], F32)
         y3 = keep.tile([P, BLOCKS, POS], F32)
@@ -184,7 +177,7 @@ def tile_lowrankconv3d_w_kernel(
         nc.scalar.activation(out=per_rank[:], in_=vectors_turned[:, 0:PACK, 0 : 3 * AXIS_ROWS], func=COPY)
         nc.vector.tensor_copy(out=per_channel[:], in_=vectors_turned[:, PACK, 0:BLOCKS])
         turned = [turn_three_ways(by_byte)]
-        products = [first_product(1)]
+        products = [y0, first_product(1), first_product(2)]
 
         def middle_tap(dst, src, axis, i):
             g, t = divmod(i, PACK)
@@ -204,17 +197,6 @@ def tile_lowrankconv3d_w_kernel(
                 outer_tap(to[:, :, step:run], frm[:, :, 0 : run - step], axis, k, i)
             else:
                 outer_tap(to[:, :, 0 : run - step], frm[:, :, step:run], axis, k, i)
-
-        def blocks_of(entry_round):
-            g, r = divmod(entry_round, ENTRY_PERIOD)
-            if not (0 <= g < GROUPS and r < ENTRY_ROUNDS):
-                return []
-            first = PACK * g + PER_ROUND * r
-            return list(range(first, first + PER_ROUND))
-
-        def group_ending(entry_round):
-            g, r = divmod(entry_round, ENTRY_PERIOD)
-            return g if 0 <= g < GROUPS and r == ENTRY_ROUNDS - 1 else None
 
         early = keep.tile([P, GROUPS, PER_BANK, POS], F32)
 
@@ -242,45 +224,48 @@ def tile_lowrankconv3d_w_kernel(
                 )
 
         early_banks = []
-        quantised = set()
 
-        for j in range(ENTRY_PERIOD * (GROUPS - 1) + ENTRY_ROUNDS + 5):
-            for i in blocks_of(j - 4):
-                middle_tap(y3[:, i, :], y2[:, i, :], AXIS_H, i)
-            for i in blocks_of(j - 2):
-                middle_tap(y2[:, i, :], y1[:, i, :], AXIS_W, i)
-            for i in blocks_of(j):
-                g, t = divmod(i, PACK)
-                middle_tap(y1[:, i, :], turned[g][0][:, t, :], AXIS_D, i)
-            g = group_ending(j - 6)
-            if g is not None and g < GROUPS - 1:
-                nc.scalar.copy(out=y3_grouped[:, g], in_=y3[:, PACK * g : PACK * (g + 1), :].rearrange("p t n -> p n t"))
-            for k in (0, 2):
-                for i in blocks_of(j - 5):
-                    outer_tap_in_sbuf(y3, y2, AXIS_H, k, i, W * D, H)
-                for i in blocks_of(j - 3):
-                    outer_tap_in_sbuf(y2, y1, AXIS_W, k, i, D, W)
-                for i in blocks_of(j - 1):
-                    g, t = divmod(i, PACK)
-                    block, place = divmod(t, PER_ROUND)
-                    outer_tap(y1[:, i, :], turned[g][1][block][:, place, k // 2, :], AXIS_D, k, i)
-            g = group_ending(j - 7)
-            if g is not None and g < GROUPS - 1:
-                nc.vector.quantize_mx(
-                    out=y3_words[:, g, :].bitcast(FP8X4),
-                    scales=y3_scales[:, g, :],
-                    in_=y3_grouped[:, g].rearrange("p n t -> p (n t)"),
+        for g in range(GROUPS):
+            blocks = range(PACK * g, PACK * (g + 1))
+            plain, below, above = turned[g]
+
+            for t, i in enumerate(blocks):
+                middle_tap(y1[:, i, :], plain[:, t, :], AXIS_D, i)
+            if g > 0:
+                nc.scalar.copy(
+                    out=y3_grouped[:, g - 1],
+                    in_=y3[:, PACK * (g - 1) : PACK * g, :].rearrange("p t n -> p n t"),
                 )
-                quantised.add(g)
+            for k, bank in ((0, below), (2, above)):
+                for t, i in enumerate(blocks):
+                    outer_tap(y1[:, i, :], bank[:, t, :], AXIS_D, k, i)
+            if g > 0:
+                nc.vector.quantize_mx(
+                    out=y3_words[:, g - 1, :].bitcast(FP8X4),
+                    scales=y3_scales[:, g - 1, :],
+                    in_=y3_grouped[:, g - 1].rearrange("p n t -> p (n t)"),
+                )
                 for q in range(GROUPS):
-                    passes = range(EARLY_PASSES[q])
-                    if g in passes and all(n in quantised for n in passes):
-                        early_banks.append((q, channel_bank(q, passes)))
-            g, r = divmod(j, ENTRY_PERIOD)
-            if r == TURN_ROUND and g + 1 < GROUPS:
-                turned.append(turn_three_ways(sort_by_byte(nc.scalar.copy, products[g])))
-                if g + 2 < GROUPS:
-                    products.append(first_product(g + 2))
+                    if EARLY_PASSES[q] == g:
+                        early_banks.append((q, channel_bank(q, range(g))))
+
+            for i in blocks:
+                middle_tap(y2[:, i, :], y1[:, i, :], AXIS_W, i)
+            if g + 1 < GROUPS:
+                turned.append(turn_three_ways(sort_by_byte(nc.scalar.copy, products[g + 1])))
+                if g + 1 + AHEAD < GROUPS:
+                    products.append(first_product(g + 1 + AHEAD))
+            else:
+                add_bias(*early_banks[0])
+            for k in (0, 2):
+                for i in blocks:
+                    outer_tap_in_sbuf(y2, y1, AXIS_W, k, i, D, W)
+
+            for i in blocks:
+                middle_tap(y3[:, i, :], y2[:, i, :], AXIS_H, i)
+            for k in (0, 2):
+                for i in blocks:
+                    outer_tap_in_sbuf(y3, y2, AXIS_H, k, i, W * D, H)
 
         last = GROUPS - 1
         halves = [slice(0, POS // 2), slice(POS // 2, POS)]
@@ -295,7 +280,7 @@ def tile_lowrankconv3d_w_kernel(
                 scales=y3_scales[:, last, half],
                 in_=y3_grouped[:, last, half].rearrange("p n t -> p (n t)"),
             )
-        for q, bank in early_banks:
+        for q, bank in early_banks[1:]:
             add_bias(q, bank)
 
         out_banks = out.rearrange("a (q j p) h w d -> q p j (a h w d)", p=P, j=PER_BANK)

@@ -20,11 +20,10 @@ K_PASS = P * PACK
 CHANNELS = 2048
 GROUPS = CHANNELS // K_PASS
 BLOCKS = CHANNELS // P
-AHEAD = 2
 H, W, D = 8, 4, 4
 POS = H * W * D
 TAPS = 3
-AXIS_H, AXIS_W, AXIS_D = 0, 1, 2
+AXIS_D, AXIS_W, AXIS_H = 0, 1, 2
 AXIS_ROWS = TAPS * GROUPS
 PER_BANK = K_PASS // POS
 EARLY_PASSES = (3, 3, 2, 2)
@@ -56,6 +55,7 @@ def tile_lowrankconv3d_w_kernel(
             out=x_raw[:], in_=x.rearrange("b (g p t) h w d -> p (b g) t (h w d)", p=P, t=PACK)
         )
 
+        vectors_d = keep.tile([P, K_PASS], BF16)
         vectors = keep.tile([P, K_PASS], BF16)
         bias_rows = keep.tile([P, P], BF16)
         nc.vector.memset(bias_rows[:], 0.0)
@@ -64,10 +64,14 @@ def tile_lowrankconv3d_w_kernel(
         in_planes = keep.tile([P, CHANNELS], U8, align_bytes=64)
         out_planes = keep.tile([P, CHANNELS], U8, align_bytes=64)
         nc.vector.memset(in_planes[:].bitcast(I32), 0)
-        nc.vector.memset(vectors[:], 0.0)
+        nc.vector.memset(vectors_d[:].bitcast(I32), 0)
+        nc.vector.memset(vectors[:].bitcast(I32), 0)
         nc.vector.memset(out_planes[:].bitcast(I32), 0)
         y2 = keep.tile([P, BLOCKS, POS], F32)
 
+        nc.scalar.dma_start(
+            out=vectors_d[0:AXIS_ROWS, :], in_=U_kd.rearrange("k (g c) -> (k g) c", g=GROUPS)
+        )
         load_scale_planes(nc, in_planes, U_c_in_scales)
         in_words = U_c_in_words.rearrange("k p n t -> p k (n t)")
         w_in = []
@@ -79,14 +83,13 @@ def tile_lowrankconv3d_w_kernel(
                     in_=in_words[:, first:end, PACK * K_PASS * g : PACK * K_PASS * (g + 1)].bitcast(I32),
                 )
             if g == 0:
-                for n, taps in enumerate((U_kh, U_kw, U_kd)):
+                for n, taps in enumerate((U_kw, U_kh)):
                     nc.sync.dma_start(
                         out=vectors[AXIS_ROWS * n : AXIS_ROWS * (n + 1), :],
                         in_=taps.rearrange("k (g c) -> (k g) c", g=GROUPS),
                     )
-                nc.sync.dma_start(
-                    out=bias_rows[0:BLOCKS, :], in_=bias.rearrange("(b c) -> b c", b=BLOCKS)
-                )
+            if g == 1:
+                nc.sync.dma_start(out=bias_rows[0:BLOCKS, :], in_=bias.rearrange("(b c) -> b c", b=BLOCKS))
         load_scale_planes(nc, out_planes, U_c_out_scales)
         w_out = []
         for g in range(GROUPS):
@@ -111,12 +114,16 @@ def tile_lowrankconv3d_w_kernel(
             out=from_above[:].rearrange("i (e d) -> i e d", d=D)[:, :, 0 : D - 1], in_=ident_d[:, :, 1:D]
         )
 
-        per_rank = keep.tile([P, PACK, 3 * AXIS_ROWS], F32)
+        taps_d = keep.tile([P, PACK, AXIS_ROWS], F32)
+        taps_wh = keep.tile([P, PACK, 2 * AXIS_ROWS], F32)
         per_channel = keep.tile([P, BLOCKS], F32)
 
         def tap(axis, k, g, t):
-            row = (axis * TAPS + k) * GROUPS + g
-            return per_rank[:, t, row : row + 1]
+            if axis == AXIS_D:
+                row = k * GROUPS + g
+                return taps_d[:, t, row : row + 1]
+            row = ((axis - AXIS_W) * TAPS + k) * GROUPS + g
+            return taps_wh[:, t, row : row + 1]
 
         x_grouped = keep.tile([P, GROUPS, POS, PACK], BF16, align_bytes=64)
         x_words = keep.tile([P, GROUPS, POS], U32, align_bytes=64)
@@ -168,16 +175,17 @@ def tile_lowrankconv3d_w_kernel(
         y3 = keep.tile([P, BLOCKS, POS], F32)
         y3_grouped = keep.tile([P, GROUPS, POS, PACK], BF16, align_bytes=64)
 
-        y0 = first_product(0)
-        vectors_turned = banks.tile([P, PACK + 1, P], BF16, tag="bank")
+        vectors_turned = banks.tile([P, PACK, P], BF16, tag="bank")
+        for t in range(PACK):
+            nc.tensor.transpose(vectors_turned[:, t, :], vectors_d[:, t:K_PASS:PACK], ident_bf[:])
+        nc.vector.tensor_copy(out=taps_d[:], in_=vectors_turned[:, :, 0:AXIS_ROWS])
+
+        product = first_product(0)
+        vectors_turned = banks.tile([P, PACK, P], BF16, tag="bank")
         for t in range(PACK):
             nc.tensor.transpose(vectors_turned[:, t, :], vectors[:, t:K_PASS:PACK], ident_bf[:])
-        nc.tensor.transpose(vectors_turned[:, PACK, :], bias_rows[:], ident_bf[:])
-        by_byte = sort_by_byte(nc.scalar.copy, y0)
-        nc.scalar.activation(out=per_rank[:], in_=vectors_turned[:, 0:PACK, 0 : 3 * AXIS_ROWS], func=COPY)
-        nc.vector.tensor_copy(out=per_channel[:], in_=vectors_turned[:, PACK, 0:BLOCKS])
-        turned = [turn_three_ways(by_byte)]
-        products = [y0, first_product(1), first_product(2)]
+        turned = [turn_three_ways(sort_by_byte(nc.scalar.copy, product))]
+        product = first_product(1)
 
         def middle_tap(dst, src, axis, i):
             g, t = divmod(i, PACK)
@@ -225,47 +233,77 @@ def tile_lowrankconv3d_w_kernel(
 
         early_banks = []
 
-        for g in range(GROUPS):
-            blocks = range(PACK * g, PACK * (g + 1))
-            plain, below, above = turned[g]
+        stages = [(AXIS_D, 0), (AXIS_W, 0)]
+        for g in range(GROUPS - 1):
+            stages += [(AXIS_D, g + 1), (AXIS_H, g), (AXIS_W, g + 1)]
+        stages.append((AXIS_H, GROUPS - 1))
 
-            for t, i in enumerate(blocks):
-                middle_tap(y1[:, i, :], plain[:, t, :], AXIS_D, i)
-            if g > 0:
-                nc.scalar.copy(
-                    out=y3_grouped[:, g - 1],
-                    in_=y3[:, PACK * (g - 1) : PACK * g, :].rearrange("p t n -> p n t"),
-                )
-            for k, bank in ((0, below), (2, above)):
-                for t, i in enumerate(blocks):
-                    outer_tap(y1[:, i, :], bank[:, t, :], AXIS_D, k, i)
-            if g > 0:
-                nc.vector.quantize_mx(
-                    out=y3_words[:, g - 1, :].bitcast(FP8X4),
-                    scales=y3_scales[:, g - 1, :],
-                    in_=y3_grouped[:, g - 1].rearrange("p n t -> p (n t)"),
-                )
-                for q in range(GROUPS):
-                    if EARLY_PASSES[q] == g:
-                        early_banks.append((q, channel_bank(q, range(g))))
+        def middle_taps(axis, g):
+            for t in range(PACK):
+                i = PACK * g + t
+                if axis == AXIS_D:
+                    middle_tap(y1[:, i, :], turned[g][0][:, t, :], axis, i)
+                elif axis == AXIS_W:
+                    middle_tap(y2[:, i, :], y1[:, i, :], axis, i)
+                else:
+                    middle_tap(y3[:, i, :], y2[:, i, :], axis, i)
 
-            for i in blocks:
-                middle_tap(y2[:, i, :], y1[:, i, :], AXIS_W, i)
-            if g + 1 < GROUPS:
-                turned.append(turn_three_ways(sort_by_byte(nc.scalar.copy, products[g + 1])))
-                if g + 1 + AHEAD < GROUPS:
-                    products.append(first_product(g + 1 + AHEAD))
-            else:
+        def outer_taps(axis, g):
+            for k in (0, 2):
+                for t in range(PACK):
+                    i = PACK * g + t
+                    if axis == AXIS_D:
+                        outer_tap(y1[:, i, :], turned[g][1 + k // 2][:, t, :], axis, k, i)
+                    elif axis == AXIS_W:
+                        outer_tap_in_sbuf(y2, y1, axis, k, i, D, W)
+                    else:
+                        outer_tap_in_sbuf(y3, y2, axis, k, i, W * D, H)
+
+        def round_group(g):
+            nc.scalar.copy(
+                out=y3_grouped[:, g], in_=y3[:, PACK * g : PACK * (g + 1), :].rearrange("p t n -> p n t")
+            )
+
+        def quantise_group(g):
+            nc.vector.quantize_mx(
+                out=y3_words[:, g, :].bitcast(FP8X4),
+                scales=y3_scales[:, g, :],
+                in_=y3_grouped[:, g].rearrange("p n t -> p (n t)"),
+            )
+            for q in range(GROUPS):
+                if EARLY_PASSES[q] == g + 1:
+                    early_banks.append((q, channel_bank(q, range(g + 1))))
+
+        for axis, g in stages:
+            middle_taps(axis, g)
+            to_turn = None
+            if (axis, g) == (AXIS_D, 0):
+                nc.scalar.activation(
+                    out=taps_wh[:], in_=vectors_turned[:, 0:PACK, 0 : 2 * AXIS_ROWS], func=COPY
+                )
+                to_turn = 1
+            if axis == AXIS_H and g + 2 < GROUPS:
+                to_turn = g + 2
+            if to_turn is not None:
+                turned.append(turn_three_ways(sort_by_byte(nc.scalar.copy, product)))
+                if to_turn == 1:
+                    bias_turned = banks.tile([P, P], BF16, tag="bank")
+                    nc.tensor.transpose(bias_turned[:], bias_rows[:], ident_bf[:])
+                if to_turn + 1 < GROUPS:
+                    product = first_product(to_turn + 1)
+            if axis == AXIS_D and g >= 2:
+                round_group(g - 2)
+            if (axis, g) == (AXIS_W, GROUPS - 1):
+                round_group(g - 1)
                 add_bias(*early_banks[0])
-            for k in (0, 2):
-                for i in blocks:
-                    outer_tap_in_sbuf(y2, y1, AXIS_W, k, i, D, W)
 
-            for i in blocks:
-                middle_tap(y3[:, i, :], y2[:, i, :], AXIS_H, i)
-            for k in (0, 2):
-                for i in blocks:
-                    outer_tap_in_sbuf(y3, y2, AXIS_H, k, i, W * D, H)
+            outer_taps(axis, g)
+            if (axis, g) == (AXIS_D, 1):
+                nc.vector.tensor_copy(out=per_channel[:], in_=bias_turned[:, 0:BLOCKS])
+            if axis == AXIS_D and g >= 2:
+                quantise_group(g - 2)
+            if (axis, g) == (AXIS_W, GROUPS - 1):
+                quantise_group(g - 1)
 
         last = GROUPS - 1
         halves = [slice(0, POS // 2), slice(POS // 2, POS)]

@@ -23,10 +23,11 @@ BLOCKS = CHANNELS // P
 H, W, D = 8, 4, 4
 POS = H * W * D
 TAPS = 3
-AXIS_D, AXIS_W, AXIS_H = 0, 1, 2
+AXIS_H, AXIS_W, AXIS_D = 0, 1, 2
 AXIS_ROWS = TAPS * GROUPS
 PER_BANK = K_PASS // POS
-EARLY_PASSES = (3, 3, 2, 2)
+EARLY_PASSES = (3, 3, 2)
+SCALAR_BANK = len(EARLY_PASSES)
 
 FLOPS = 2 * 2 * POS * CHANNELS * CHANNELS + 2 * 3 * TAPS * POS * CHANNELS
 
@@ -55,7 +56,7 @@ def tile_lowrankconv3d_w_kernel(
             out=x_raw[:], in_=x.rearrange("b (g p t) h w d -> p (b g) t (h w d)", p=P, t=PACK)
         )
 
-        vectors_d = keep.tile([P, K_PASS], BF16)
+        vectors_h = keep.tile([P, K_PASS], BF16)
         vectors = keep.tile([P, K_PASS], BF16)
         bias_rows = keep.tile([P, P], BF16)
         nc.vector.memset(bias_rows[:], 0.0)
@@ -64,13 +65,13 @@ def tile_lowrankconv3d_w_kernel(
         in_planes = keep.tile([P, CHANNELS], U8, align_bytes=64)
         out_planes = keep.tile([P, CHANNELS], U8, align_bytes=64)
         nc.vector.memset(in_planes[:].bitcast(I32), 0)
-        nc.vector.memset(vectors_d[:].bitcast(I32), 0)
+        nc.vector.memset(vectors_h[:].bitcast(I32), 0)
         nc.vector.memset(vectors[:].bitcast(I32), 0)
         nc.vector.memset(out_planes[:].bitcast(I32), 0)
         y2 = keep.tile([P, BLOCKS, POS], F32)
 
         nc.scalar.dma_start(
-            out=vectors_d[0:AXIS_ROWS, :], in_=U_kd.rearrange("k (g c) -> (k g) c", g=GROUPS)
+            out=vectors_h[0:AXIS_ROWS, :], in_=U_kh.rearrange("k (g c) -> (k g) c", g=GROUPS)
         )
         load_scale_planes(nc, in_planes, U_c_in_scales)
         in_words = U_c_in_words.rearrange("k p n t -> p k (n t)")
@@ -82,13 +83,12 @@ def tile_lowrankconv3d_w_kernel(
                     out=w_in[g][:, first:end, :],
                     in_=in_words[:, first:end, PACK * K_PASS * g : PACK * K_PASS * (g + 1)].bitcast(I32),
                 )
-            if g == 0:
-                for n, taps in enumerate((U_kw, U_kh)):
+            if g == 1:
+                for n, taps in enumerate((U_kw, U_kd)):
                     nc.sync.dma_start(
                         out=vectors[AXIS_ROWS * n : AXIS_ROWS * (n + 1), :],
                         in_=taps.rearrange("k (g c) -> (k g) c", g=GROUPS),
                     )
-            if g == 1:
                 nc.sync.dma_start(out=bias_rows[0:BLOCKS, :], in_=bias.rearrange("(b c) -> b c", b=BLOCKS))
         load_scale_planes(nc, out_planes, U_c_out_scales)
         w_out = []
@@ -102,28 +102,40 @@ def tile_lowrankconv3d_w_kernel(
         make_identity(nc, ident_bf[:])
         ident = keep.tile([P, P], F32)
         make_identity(nc, ident[:])
+
+        plain = keep.tile([P, POS], F32)
         from_below = keep.tile([P, POS], F32)
         from_above = keep.tile([P, POS], F32)
         nc.vector.memset(from_below[:], 0.0)
         nc.vector.memset(from_above[:], 0.0)
-        ident_d = ident[:].rearrange("i (e d) -> i e d", d=D)
         nc.vector.tensor_copy(
-            out=from_below[:].rearrange("i (e d) -> i e d", d=D)[:, :, 1:D], in_=ident_d[:, :, 0 : D - 1]
+            out=plain[:].rearrange("i (d w h) -> i d w h", d=D, w=W),
+            in_=ident[:].rearrange("i (h w d) -> i d w h", h=H, w=W),
+        )
+        plain_h = plain[:].rearrange("i (e h) -> i e h", h=H)
+        nc.vector.tensor_copy(
+            out=from_below[:].rearrange("i (e h) -> i e h", h=H)[:, :, 1:H], in_=plain_h[:, :, 0 : H - 1]
         )
         nc.vector.tensor_copy(
-            out=from_above[:].rearrange("i (e d) -> i e d", d=D)[:, :, 0 : D - 1], in_=ident_d[:, :, 1:D]
+            out=from_above[:].rearrange("i (e h) -> i e h", h=H)[:, :, 0 : H - 1], in_=plain_h[:, :, 1:H]
         )
 
-        taps_d = keep.tile([P, PACK, AXIS_ROWS], F32)
-        taps_wh = keep.tile([P, PACK, 2 * AXIS_ROWS], F32)
+        def natural(sums):
+            return sums.rearrange("p (d w h) -> p h w d", d=D, w=W)
+
+        def by_axes(result):
+            return result.rearrange("p (h w d) -> p h w d", h=H, w=W)
+
+        taps_h = keep.tile([P, PACK, AXIS_ROWS], F32)
+        taps_wd = keep.tile([P, PACK, 2 * AXIS_ROWS], F32)
         per_channel = keep.tile([P, BLOCKS], F32)
 
         def tap(axis, k, g, t):
-            if axis == AXIS_D:
+            if axis == AXIS_H:
                 row = k * GROUPS + g
-                return taps_d[:, t, row : row + 1]
+                return taps_h[:, t, row : row + 1]
             row = ((axis - AXIS_W) * TAPS + k) * GROUPS + g
-            return taps_wh[:, t, row : row + 1]
+            return taps_wd[:, t, row : row + 1]
 
         x_grouped = keep.tile([P, GROUPS, POS, PACK], BF16, align_bytes=64)
         x_words = keep.tile([P, GROUPS, POS], U32, align_bytes=64)
@@ -164,7 +176,7 @@ def tile_lowrankconv3d_w_kernel(
 
         def turn_three_ways(by_byte):
             three_banks = []
-            for matrix in (ident, from_below, from_above):
+            for matrix in (plain, from_below, from_above):
                 bank = banks.tile([P, PACK, POS], F32, tag="bank")
                 for t in range(PACK):
                     nc.tensor.transpose(bank[:, t, :], by_byte[:, t, :], matrix[:])
@@ -175,17 +187,19 @@ def tile_lowrankconv3d_w_kernel(
         y3 = keep.tile([P, BLOCKS, POS], F32)
         y3_grouped = keep.tile([P, GROUPS, POS, PACK], BF16, align_bytes=64)
 
-        vectors_turned = banks.tile([P, PACK, P], BF16, tag="bank")
-        for t in range(PACK):
-            nc.tensor.transpose(vectors_turned[:, t, :], vectors_d[:, t:K_PASS:PACK], ident_bf[:])
-        nc.vector.tensor_copy(out=taps_d[:], in_=vectors_turned[:, :, 0:AXIS_ROWS])
+        def turn_taps(bank, rows):
+            for t in range(PACK):
+                nc.tensor.transpose(bank[:, t, :], rows[:, t:K_PASS:PACK], ident_bf[:])
 
         product = first_product(0)
-        vectors_turned = banks.tile([P, PACK, P], BF16, tag="bank")
-        for t in range(PACK):
-            nc.tensor.transpose(vectors_turned[:, t, :], vectors[:, t:K_PASS:PACK], ident_bf[:])
+        h_turned = banks.tile([P, PACK, P], BF16, tag="bank")
+        turn_taps(h_turned, vectors_h)
+        nc.vector.tensor_copy(out=taps_h[:], in_=h_turned[:, :, 0:AXIS_ROWS])
         turned = [turn_three_ways(sort_by_byte(nc.scalar.copy, product))]
         product = first_product(1)
+        rest_turned = banks.tile([P, PACK + 1, P], BF16, tag="bank")
+        turn_taps(rest_turned, vectors)
+        nc.tensor.transpose(rest_turned[:, PACK, :], bias_rows[:], ident_bf[:])
 
         def middle_tap(dst, src, axis, i):
             g, t = divmod(i, PACK)
@@ -206,42 +220,52 @@ def tile_lowrankconv3d_w_kernel(
             else:
                 outer_tap(to[:, :, 0 : run - step], frm[:, :, step:run], axis, k, i)
 
-        early = keep.tile([P, GROUPS, PER_BANK, POS], F32)
+        early = keep.tile([P, SCALAR_BANK, PER_BANK, POS], F32)
+
+        def multiply(sums, b, g, start, stop):
+            nc.tensor.matmul_mx(
+                out=sums,
+                lhsT=w_out[g][:, P * b : P * (b + 1)].bitcast(FP8X4),
+                lhsT_scale=out_planes[PACK * g : P, P * b : P * (b + 1)],
+                rhs=y3_words[:, g, :].bitcast(FP8X4),
+                rhs_scale=y3_scales[:, g, :],
+                start=start,
+                stop=stop,
+            )
 
         def channel_bank(q, passes):
             bank = banks.tile([P, PER_BANK, POS], F32, tag="bank")
             for j in range(PER_BANK):
-                first = P * (PER_BANK * q + j)
                 for g in passes:
-                    nc.tensor.matmul_mx(
-                        out=bank[:, j, :],
-                        lhsT=w_out[g][:, first : first + P].bitcast(FP8X4),
-                        lhsT_scale=out_planes[PACK * g : P, first : first + P],
-                        rhs=y3_words[:, g, :].bitcast(FP8X4),
-                        rhs_scale=y3_scales[:, g, :],
-                        start=(g == passes[0]),
-                        stop=(g == passes[-1]),
-                    )
+                    multiply(bank[:, j, :], PER_BANK * q + j, g, g == passes[0], g == passes[-1])
             return bank
 
-        def add_bias(q, bank):
+        open_banks = []
+
+        def multiply_open(g):
             for j in range(PER_BANK):
-                b = PER_BANK * q + j
-                nc.scalar.activation(
-                    out=early[:, q, j, :], in_=bank[:, j, :], func=IDENTITY, bias=per_channel[:, b : b + 1]
-                )
+                multiply(open_banks[j][:, 0:POS], PER_BANK * SCALAR_BANK + j, g, g == 0, g == GROUPS - 1)
+
+        def add_bias(dst, src, b):
+            nc.scalar.activation(
+                out=by_axes(dst), in_=natural(src), func=IDENTITY, bias=per_channel[:, b : b + 1]
+            )
+
+        def empty_early_bank(q, bank):
+            for j in range(PER_BANK):
+                add_bias(early[:, q, j, :], bank[:, j, :], PER_BANK * q + j)
 
         early_banks = []
 
-        stages = [(AXIS_D, 0), (AXIS_W, 0)]
+        stages = [(AXIS_H, 0), (AXIS_W, 0)]
         for g in range(GROUPS - 1):
-            stages += [(AXIS_D, g + 1), (AXIS_H, g), (AXIS_W, g + 1)]
-        stages.append((AXIS_H, GROUPS - 1))
+            stages += [(AXIS_H, g + 1), (AXIS_D, g), (AXIS_W, g + 1)]
+        stages.append((AXIS_D, GROUPS - 1))
 
         def middle_taps(axis, g):
             for t in range(PACK):
                 i = PACK * g + t
-                if axis == AXIS_D:
+                if axis == AXIS_H:
                     middle_tap(y1[:, i, :], turned[g][0][:, t, :], axis, i)
                 elif axis == AXIS_W:
                     middle_tap(y2[:, i, :], y1[:, i, :], axis, i)
@@ -252,12 +276,12 @@ def tile_lowrankconv3d_w_kernel(
             for k in (0, 2):
                 for t in range(PACK):
                     i = PACK * g + t
-                    if axis == AXIS_D:
+                    if axis == AXIS_H:
                         outer_tap(y1[:, i, :], turned[g][1 + k // 2][:, t, :], axis, k, i)
                     elif axis == AXIS_W:
-                        outer_tap_in_sbuf(y2, y1, axis, k, i, D, W)
+                        outer_tap_in_sbuf(y2, y1, axis, k, i, H, W)
                     else:
-                        outer_tap_in_sbuf(y3, y2, axis, k, i, W * D, H)
+                        outer_tap_in_sbuf(y3, y2, axis, k, i, W * H, D)
 
         def round_group(g):
             nc.scalar.copy(
@@ -270,37 +294,37 @@ def tile_lowrankconv3d_w_kernel(
                 scales=y3_scales[:, g, :],
                 in_=y3_grouped[:, g].rearrange("p n t -> p (n t)"),
             )
-            for q in range(GROUPS):
+            if g == 1:
+                for n in range(PER_BANK):
+                    open_banks.append(banks.tile([P, K_PASS], F32, name="open%d" % n, tag="bank"))
+                multiply_open(0)
+            if g >= 1:
+                multiply_open(g)
+            for q in range(SCALAR_BANK):
                 if EARLY_PASSES[q] == g + 1:
                     early_banks.append((q, channel_bank(q, range(g + 1))))
 
         for axis, g in stages:
+            if (axis, g) == (AXIS_W, 0):
+                nc.scalar.activation(out=taps_wd[:], in_=rest_turned[:, 0:PACK, 0 : 2 * AXIS_ROWS], func=COPY)
             middle_taps(axis, g)
-            to_turn = None
-            if (axis, g) == (AXIS_D, 0):
-                nc.scalar.activation(
-                    out=taps_wh[:], in_=vectors_turned[:, 0:PACK, 0 : 2 * AXIS_ROWS], func=COPY
-                )
-                to_turn = 1
-            if axis == AXIS_H and g + 2 < GROUPS:
+            to_turn = 1 if (axis, g) == (AXIS_H, 0) else None
+            if axis == AXIS_D and g + 2 < GROUPS:
                 to_turn = g + 2
             if to_turn is not None:
                 turned.append(turn_three_ways(sort_by_byte(nc.scalar.copy, product)))
-                if to_turn == 1:
-                    bias_turned = banks.tile([P, P], BF16, tag="bank")
-                    nc.tensor.transpose(bias_turned[:], bias_rows[:], ident_bf[:])
                 if to_turn + 1 < GROUPS:
                     product = first_product(to_turn + 1)
-            if axis == AXIS_D and g >= 2:
+            if axis == AXIS_H and g >= 2:
                 round_group(g - 2)
             if (axis, g) == (AXIS_W, GROUPS - 1):
                 round_group(g - 1)
-                add_bias(*early_banks[0])
+                empty_early_bank(*early_banks[0])
 
             outer_taps(axis, g)
-            if (axis, g) == (AXIS_D, 1):
-                nc.vector.tensor_copy(out=per_channel[:], in_=bias_turned[:, 0:BLOCKS])
-            if axis == AXIS_D and g >= 2:
+            if (axis, g) == (AXIS_H, 1):
+                nc.vector.tensor_copy(out=per_channel[:], in_=rest_turned[:, PACK, 0:BLOCKS])
+            if axis == AXIS_H and g >= 2:
                 quantise_group(g - 2)
             if (axis, g) == (AXIS_W, GROUPS - 1):
                 quantise_group(g - 1)
@@ -319,11 +343,28 @@ def tile_lowrankconv3d_w_kernel(
                 in_=y3_grouped[:, last, half].rearrange("p n t -> p (n t)"),
             )
         for q, bank in early_banks[1:]:
-            add_bias(q, bank)
+            empty_early_bank(q, bank)
 
         out_banks = out.rearrange("a (q j p) h w d -> q p j (a h w d)", p=P, j=PER_BANK)
-        for q in range(GROUPS):
+
+        def finish_on_vector(q):
             rest = channel_bank(q, range(EARLY_PASSES[q], GROUPS))
             result = results.tile([P, PER_BANK, POS], F32)
-            nc.vector.tensor_tensor(out=result[:], in0=rest[:], in1=early[:, q], op=ADD)
-            nc.sync.dma_start(out=out_banks[q], in_=result[:])
+            step = PER_BANK // 2 if q == SCALAR_BANK - 1 else PER_BANK
+            for first in range(0, PER_BANK, step):
+                for j in range(first, first + step):
+                    nc.vector.tensor_tensor(
+                        out=by_axes(result[:, j]), in0=natural(rest[:, j]), in1=by_axes(early[:, q, j]), op=ADD
+                    )
+                nc.sync.dma_start(
+                    out=out_banks[q][:, first : first + step], in_=result[:, first : first + step]
+                )
+
+        finish_on_vector(0)
+        multiply_open(last)
+        result = results.tile([P, PER_BANK, POS], F32)
+        for n in range(PER_BANK):
+            add_bias(result[:, n, :], open_banks[n][:, 0:POS], PER_BANK * SCALAR_BANK + n)
+        nc.sync.dma_start(out=out_banks[SCALAR_BANK], in_=result[:])
+        for q in range(1, SCALAR_BANK):
+            finish_on_vector(q)

from contextlib import ExitStack

import concourse.mybir as mybir
from concourse.masks import make_identity

F32 = mybir.dt.float32
BF16 = mybir.dt.bfloat16
I32 = mybir.dt.int32
U32 = mybir.dt.uint32
U8 = mybir.dt.uint8
FP8X4 = mybir.dt.float8_e4m3fn_x4
MULT = mybir.AluOpType.mult
ADD = mybir.AluOpType.add
COPY = mybir.ActivationFunctionType.Copy
IDENTITY = mybir.ActivationFunctionType.Identity

P = 128
PACK = 4
K_PASS = P * PACK
CHANNELS = 2048
GROUPS = CHANNELS // K_PASS
BLOCKS = CHANNELS // P
H, W, D = 8, 4, 4
POS = H * W * D
TAPS = 3
AXIS_H, AXIS_W, AXIS_D = 0, 1, 2
AXIS_ROWS = TAPS * GROUPS
PER_BANK = K_PASS // POS
EARLY_PASSES = (3, 3, 2)
SCALAR_BANK = len(EARLY_PASSES)

FLOPS = 2 * 2 * POS * CHANNELS * CHANNELS + 2 * 3 * TAPS * POS * CHANNELS


def load_scale_planes(nc, planes, scales):
    for quad in range(4):
        nc.sync.dma_start(
            out=planes[32 * quad : 32 * quad + 16, :].bitcast(I32),
            in_=scales[:, 4 * quad : 4 * quad + 4, :].bitcast(I32),
        )


def tile_lowrankconv3d_w_kernel(
    tc, x, U_kh, U_kw, U_kd, U_c_in_words, U_c_in_scales, U_c_out_words, U_c_out_scales, bias, out
):
    nc = tc.nc
    with ExitStack() as ctx:
        keep = ctx.enter_context(tc.tile_pool(name="keep", bufs=1))
        work = ctx.enter_context(tc.tile_pool(name="work", bufs=2))
        results = ctx.enter_context(tc.tile_pool(name="results", bufs=GROUPS))
        banks = ctx.enter_context(tc.psum_pool(name="banks", bufs=8))
        ctx.enter_context(tc.manual_schedule())

        x_raw = keep.tile([P, GROUPS, PACK, POS], BF16)
        nc.sync.dma_start(
            out=x_raw[:], in_=x.rearrange("b (g p t) h w d -> p (b g) t (h w d)", p=P, t=PACK)
        )

        vectors_h = keep.tile([P, K_PASS], BF16)
        vectors = keep.tile([P, K_PASS], BF16)
        bias_rows = keep.tile([P, P], BF16)
        nc.vector.memset(bias_rows[:], 0.0)
        loaded = keep.tile([P, 1], F32)
        nc.scalar.activation(out=loaded[:], in_=bias_rows[:, 0:1], func=COPY)
        in_planes = keep.tile([P, CHANNELS], U8, align_bytes=64)
        out_planes = keep.tile([P, CHANNELS], U8, align_bytes=64)
        nc.vector.memset(in_planes[:].bitcast(I32), 0)
        nc.vector.memset(vectors_h[:].bitcast(I32), 0)
        nc.vector.memset(vectors[:].bitcast(I32), 0)
        nc.vector.memset(out_planes[:].bitcast(I32), 0)
        y2 = keep.tile([P, BLOCKS, POS], F32)

        nc.scalar.dma_start(
            out=vectors_h[0:AXIS_ROWS, :], in_=U_kh.rearrange("k (g c) -> (k g) c", g=GROUPS)
        )
        load_scale_planes(nc, in_planes, U_c_in_scales)
        in_words = U_c_in_words.rearrange("k p n t -> p k (n t)")
        w_in = []
        for g in range(GROUPS):
            w_in.append(keep.tile([P, GROUPS, K_PASS], I32, name="w_in%d" % g, align_bytes=64))
            for first, end in ((0, 1), (1, 2), (2, 4)) if g == 0 else ((0, 2), (2, 4)):
                nc.sync.dma_start(
                    out=w_in[g][:, first:end, :],
                    in_=in_words[:, first:end, PACK * K_PASS * g : PACK * K_PASS * (g + 1)].bitcast(I32),
                )
            if g == 1:
                for n, taps in enumerate((U_kw, U_kd)):
                    nc.sync.dma_start(
                        out=vectors[AXIS_ROWS * n : AXIS_ROWS * (n + 1), :],
                        in_=taps.rearrange("k (g c) -> (k g) c", g=GROUPS),
                    )
                nc.sync.dma_start(out=bias_rows[0:BLOCKS, :], in_=bias.rearrange("(b c) -> b c", b=BLOCKS))
        load_scale_planes(nc, out_planes, U_c_out_scales)
        w_out = []
        for g in range(GROUPS):
            w_out.append(keep.tile([P, CHANNELS], I32, name="w_out%d" % g, align_bytes=64))
            nc.sync.dma_start(
                out=w_out[g][:], in_=U_c_out_words[g].rearrange("p n t -> p (n t)").bitcast(I32)
            )

        ident_bf = keep.tile([P, P], BF16)
        make_identity(nc, ident_bf[:])
        ident = keep.tile([P, P], F32)
        make_identity(nc, ident[:])

        plain = keep.tile([P, POS], F32)
        from_below = keep.tile([P, POS], F32)
        from_above = keep.tile([P, POS], F32)
        nc.vector.memset(from_below[:], 0.0)
        nc.vector.memset(from_above[:], 0.0)
        nc.vector.tensor_copy(
            out=plain[:].rearrange("i (d w h) -> i d w h", d=D, w=W),
            in_=ident[:].rearrange("i (h w d) -> i d w h", h=H, w=W),
        )
        plain_h = plain[:].rearrange("i (e h) -> i e h", h=H)
        nc.vector.tensor_copy(
            out=from_below[:].rearrange("i (e h) -> i e h", h=H)[:, :, 1:H], in_=plain_h[:, :, 0 : H - 1]
        )
        nc.vector.tensor_copy(
            out=from_above[:].rearrange("i (e h) -> i e h", h=H)[:, :, 0 : H - 1], in_=plain_h[:, :, 1:H]
        )

        def natural(sums):
            return sums.rearrange("p (d w h) -> p h w d", d=D, w=W)

        def by_axes(result):
            return result.rearrange("p (h w d) -> p h w d", h=H, w=W)

        taps_h = keep.tile([P, PACK, AXIS_ROWS], F32)
        taps_wd = keep.tile([P, PACK, 2 * AXIS_ROWS], F32)
        per_channel = keep.tile([P, BLOCKS], F32)

        def tap(axis, k, g, t):
            if axis == AXIS_H:
                row = k * GROUPS + g
                return taps_h[:, t, row : row + 1]
            row = ((axis - AXIS_W) * TAPS + k) * GROUPS + g
            return taps_wd[:, t, row : row + 1]

        x_grouped = keep.tile([P, GROUPS, POS, PACK], BF16, align_bytes=64)
        x_words = keep.tile([P, GROUPS, POS], U32, align_bytes=64)
        x_scales = keep.tile([P, GROUPS, POS], U8, align_bytes=64)
        for k in range(GROUPS + 1):
            if k < GROUPS:
                nc.vector.tensor_copy(
                    out=x_grouped[:, k], in_=x_raw[:, k].rearrange("p t n -> p n t")
                )
            if k > 0:
                nc.vector.quantize_mx(
                    out=x_words[:, k - 1, :].bitcast(FP8X4),
                    scales=x_scales[:, k - 1, :],
                    in_=x_grouped[:, k - 1].rearrange("p n t -> p (n t)"),
                )

        y3_words = keep.tile([P, GROUPS, POS], U32, align_bytes=64)
        y3_scales = keep.tile([P, GROUPS, POS], U8, align_bytes=64)

        def sort_by_byte(copy, bank):
            by_byte = work.tile([P, PACK, P], F32, tag="by_byte")
            copy(out=by_byte[:], in_=bank[:].rearrange("n (p t) -> n t p", t=PACK))
            return by_byte

        def first_product(g):
            y0 = banks.tile([P, K_PASS], F32, tag="bank")
            for k in range(GROUPS):
                nc.tensor.matmul_mx(
                    out=y0[:],
                    lhsT=x_words[:, k, :].bitcast(FP8X4),
                    lhsT_scale=x_scales[:, k, :],
                    rhs=w_in[g][:, k, :].bitcast(FP8X4),
                    rhs_scale=in_planes[PACK * k : P, K_PASS * g : K_PASS * (g + 1)],
                    start=(k == 0),
                    stop=(k == GROUPS - 1),
                )
            return y0

        def turn_three_ways(by_byte):
            three_banks = []
            for matrix in (plain, from_below, from_above):
                bank = banks.tile([P, PACK, POS], F32, tag="bank")
                for t in range(PACK):
                    nc.tensor.transpose(bank[:, t, :], by_byte[:, t, :], matrix[:])
                three_banks.append(bank)
            return three_banks

        y1 = keep.tile([P, BLOCKS, POS], F32)
        y3 = keep.tile([P, BLOCKS, POS], F32)
        y3_grouped = keep.tile([P, GROUPS, POS, PACK], BF16, align_bytes=64)

        def turn_taps(bank, rows):
            for t in range(PACK):
                nc.tensor.transpose(bank[:, t, :], rows[:, t:K_PASS:PACK], ident_bf[:])

        product = first_product(0)
        h_turned = banks.tile([P, PACK, P], BF16, tag="bank")
        turn_taps(h_turned, vectors_h)
        nc.vector.tensor_copy(out=taps_h[:], in_=h_turned[:, :, 0:AXIS_ROWS])
        turned = [turn_three_ways(sort_by_byte(nc.scalar.copy, product))]
        product = first_product(1)
        rest_turned = banks.tile([P, PACK + 1, P], BF16, tag="bank")
        turn_taps(rest_turned, vectors)
        nc.tensor.transpose(rest_turned[:, PACK, :], bias_rows[:], ident_bf[:])

        def middle_tap(dst, src, axis, i):
            g, t = divmod(i, PACK)
            nc.scalar.activation(out=dst, in_=src, func=COPY, scale=tap(axis, 1, g, t))

        def outer_tap(dst, src, axis, k, i):
            g, t = divmod(i, PACK)
            nc.vector.scalar_tensor_tensor(
                out=dst, in0=src, scalar=tap(axis, k, g, t), in1=dst, op0=MULT, op1=ADD
            )

        def outer_tap_in_sbuf(dst, src, axis, k, i, step, length):
            run = step * length
            to = dst[:, i, :].rearrange("p (a e) -> p a e", e=run)
            frm = src[:, i, :].rearrange("p (a e) -> p a e", e=run)
            if k == 0:
                outer_tap(to[:, :, step:run], frm[:, :, 0 : run - step], axis, k, i)
            else:
                outer_tap(to[:, :, 0 : run - step], frm[:, :, step:run], axis, k, i)

        early = keep.tile([P, SCALAR_BANK, PER_BANK, POS], F32)

        def multiply(sums, b, g, start, stop):
            nc.tensor.matmul_mx(
                out=sums,
                lhsT=w_out[g][:, P * b : P * (b + 1)].bitcast(FP8X4),
                lhsT_scale=out_planes[PACK * g : P, P * b : P * (b + 1)],
                rhs=y3_words[:, g, :].bitcast(FP8X4),
                rhs_scale=y3_scales[:, g, :],
                start=start,
                stop=stop,
            )

        def channel_bank(q, passes):
            bank = banks.tile([P, PER_BANK, POS], F32, tag="bank")
            for j in range(PER_BANK):
                for g in passes:
                    multiply(bank[:, j, :], PER_BANK * q + j, g, g == passes[0], g == passes[-1])
            return bank

        open_banks = []

        def multiply_open(g):
            for j in range(PER_BANK):
                multiply(open_banks[j][:, 0:POS], PER_BANK * SCALAR_BANK + j, g, g == 0, g == GROUPS - 1)

        def add_bias(dst, src, b):
            nc.scalar.activation(
                out=by_axes(dst), in_=natural(src), func=IDENTITY, bias=per_channel[:, b : b + 1]
            )

        def empty_early_bank(q, bank):
            for j in range(PER_BANK):
                add_bias(early[:, q, j, :], bank[:, j, :], PER_BANK * q + j)

        early_banks = []

        stages = [(AXIS_H, 0), (AXIS_W, 0)]
        for g in range(GROUPS - 1):
            stages += [(AXIS_H, g + 1), (AXIS_D, g), (AXIS_W, g + 1)]
        stages.append((AXIS_D, GROUPS - 1))

        def middle_taps(axis, g):
            for t in range(PACK):
                i = PACK * g + t
                if axis == AXIS_H:
                    middle_tap(y1[:, i, :], turned[g][0][:, t, :], axis, i)
                elif axis == AXIS_W:
                    middle_tap(y2[:, i, :], y1[:, i, :], axis, i)
                else:
                    middle_tap(y3[:, i, :], y2[:, i, :], axis, i)

        def outer_taps(axis, g):
            for k in (0, 2):
                for t in range(PACK):
                    i = PACK * g + t
                    if axis == AXIS_H:
                        outer_tap(y1[:, i, :], turned[g][1 + k // 2][:, t, :], axis, k, i)
                    elif axis == AXIS_W:
                        outer_tap_in_sbuf(y2, y1, axis, k, i, H, W)
                    else:
                        outer_tap_in_sbuf(y3, y2, axis, k, i, W * H, D)

        def round_group(g):
            nc.scalar.copy(
                out=y3_grouped[:, g], in_=y3[:, PACK * g : PACK * (g + 1), :].rearrange("p t n -> p n t")
            )

        def quantise_group(g):
            nc.vector.quantize_mx(
                out=y3_words[:, g, :].bitcast(FP8X4),
                scales=y3_scales[:, g, :],
                in_=y3_grouped[:, g].rearrange("p n t -> p (n t)"),
            )
            if g == 1:
                for n in range(PER_BANK):
                    open_banks.append(banks.tile([P, K_PASS], F32, name="open%d" % n, tag="bank"))
                multiply_open(0)
            if g >= 1:
                multiply_open(g)
            for q in range(SCALAR_BANK):
                if EARLY_PASSES[q] == g + 1:
                    early_banks.append((q, channel_bank(q, range(g + 1))))

        for axis, g in stages:
            if (axis, g) == (AXIS_W, 0):
                nc.scalar.activation(out=taps_wd[:], in_=rest_turned[:, 0:PACK, 0 : 2 * AXIS_ROWS], func=COPY)
            middle_taps(axis, g)
            to_turn = 1 if (axis, g) == (AXIS_H, 0) else None
            if axis == AXIS_D and g + 2 < GROUPS:
                to_turn = g + 2
            if to_turn is not None:
                turned.append(turn_three_ways(sort_by_byte(nc.scalar.copy, product)))
                if to_turn + 1 < GROUPS:
                    product = first_product(to_turn + 1)
            if axis == AXIS_H and g >= 2:
                round_group(g - 2)
            if (axis, g) == (AXIS_W, GROUPS - 1):
                round_group(g - 1)
                empty_early_bank(*early_banks[0])

            outer_taps(axis, g)
            if (axis, g) == (AXIS_H, 1):
                nc.vector.tensor_copy(out=per_channel[:], in_=rest_turned[:, PACK, 0:BLOCKS])
            if axis == AXIS_H and g >= 2:
                quantise_group(g - 2)
            if (axis, g) == (AXIS_W, GROUPS - 1):
                quantise_group(g - 1)

        last = GROUPS - 1
        halves = [slice(0, POS // 2), slice(POS // 2, POS)]
        for half in halves:
            nc.vector.tensor_copy(
                out=y3_grouped[:, last, half],
                in_=y3[:, PACK * last : PACK * GROUPS, half].rearrange("p t n -> p n t"),
            )
        for half in halves:
            nc.vector.quantize_mx(
                out=y3_words[:, last, half].bitcast(FP8X4),
                scales=y3_scales[:, last, half],
                in_=y3_grouped[:, last, half].rearrange("p n t -> p (n t)"),
            )
        for q, bank in early_banks[1:]:
            empty_early_bank(q, bank)

        out_banks = out.rearrange("a (q j p) h w d -> q p j (a h w d)", p=P, j=PER_BANK)

        def finish_on_vector(q):
            rest = channel_bank(q, range(EARLY_PASSES[q], GROUPS))
            result = results.tile([P, PER_BANK, POS], F32)
            step = PER_BANK // 2 if q == SCALAR_BANK - 1 else PER_BANK
            for first in range(0, PER_BANK, step):
                for j in range(first, first + step):
                    nc.vector.tensor_tensor(
                        out=by_axes(result[:, j]), in0=natural(rest[:, j]), in1=by_axes(early[:, q, j]), op=ADD
                    )
                nc.sync.dma_start(
                    out=out_banks[q][:, first : first + step], in_=result[:, first : first + step]
                )

        finish_on_vector(0)
        multiply_open(last)
        result = results.tile([P, PER_BANK, POS], F32)
        for n in range(PER_BANK):
            add_bias(result[:, n, :], open_banks[n][:, 0:POS], PER_BANK * SCALAR_BANK + n)
        nc.sync.dma_start(out=out_banks[SCALAR_BANK], in_=result[:])
        for q in range(1, SCALAR_BANK):
            finish_on_vector(q)
